import numpy as np
import ml_dtypes


def mxq(x, axis, fmt="e4m3"):
    dtype, down = {"e4m3": (ml_dtypes.float8_e4m3fn, 7), "e5m2": (ml_dtypes.float8_e5m2, 14)}[fmt]
    v = np.moveaxis(np.asarray(x, np.float32).astype(ml_dtypes.bfloat16).astype(np.float64), axis, -1)
    blocks = v.reshape(v.shape[:-1] + (-1, 32))
    amax = np.abs(blocks).max(-1, keepdims=True)
    byte = np.maximum(np.where(amax > 0, np.frexp(amax)[1] - 1 + 127, 0) - down, 1)
    scale = np.exp2(byte - 127.0)
    codes = (blocks / scale).astype(np.float32).astype(dtype).astype(np.float64)
    return np.moveaxis((codes * scale).reshape(v.shape), -1, axis)


WIDE = False


def mx_kscale(k):
    if not WIDE:
        return np.ones(k)
    levels = np.array([10, -10, 5, -5, 0])
    a = np.random.permutation(np.resize(levels, k // 512 * 4)).reshape(k // 512, 4)
    idx = np.arange(k)
    return np.exp2(a[idx // 512, idx % 128 // 32])


BF16 = ml_dtypes.bfloat16


def bf(x):
    return np.asarray(x, np.float32).astype(BF16)


def f64(x):
    return np.asarray(x).astype(np.float64)


B, T, HID, H, D, QB = 1, 1024, 1536, 12, 128, 512
LN_EPS = 1e-5


def layer_norm(u):
    mu = u.mean(-1, keepdims=True)
    var = ((u - mu) ** 2).mean(-1, keepdims=True)
    return (u - mu) * (1.0 / np.sqrt(var + LN_EPS))


def feature_map(u, gamma, beta):
    return layer_norm(u * gamma + beta)


def setup_inputs():
    s = mx_kscale(HID)
    return {"hidden_states": bf(np.random.standard_normal((B, T, HID)) * s),
            "Wq": bf(np.random.standard_normal((H * D, HID)) / np.sqrt(HID) / s),
            "Wk": bf(np.random.standard_normal((H * D, HID)) / np.sqrt(HID) / s),
            "gamma": bf(1.0 + 0.1 * np.random.standard_normal(D)),
            "beta": bf(0.1 * np.random.standard_normal(D))}


def reference(hidden_states, Wq, Wk, gamma, beta):
    g, b = f64(gamma), f64(beta)
    xq = mxq(f64(hidden_states), 2, "e4m3")
    q = (xq @ mxq(f64(Wq), 1, "e4m3").T).reshape(B, T, H, D)
    k = (xq @ mxq(f64(Wk), 1, "e4m3").T).reshape(B, T, H, D)
    q_feat = feature_map(q, g, b) * (D ** -0.5)
    k_feat = feature_map(k, g, b)
    return q_feat, k_feat

@@ -1,0 +1,293 @@
+from contextlib import ExitStack
+
+import concourse.mybir as mybir
+from concourse.masks import make_identity
+
+F32 = mybir.dt.float32
+BF16 = mybir.dt.bfloat16
+U32 = mybir.dt.uint32
+U8 = mybir.dt.uint8
+FP8X4 = mybir.dt.float8_e4m3fn_x4
+ALU = mybir.AluOpType
+ACT = mybir.ActivationFunctionType
+AX = mybir.AxisListType
+
+P = 128
+T = 1024
+K = 1536
+D = 128
+H = 12
+NT = T // P
+K_PASS = 512
+PASSES = K // K_PASS
+LN_EPS = 1e-5
+
+FLOPS = 2 * T * (2 * K) * K
+
+GROUPS = [(0, 0, 2), (0, 2, 2), (0, 4, 4), (0, 8, 4), (1, 0, 4), (1, 4, 4), (1, 8, 4)]
+NG = len(GROUPS)
+BATCHES = [[(0, 8)]] * (NG - 1) + [[(0, 4), (4, 6), (6, 8)]]
+LAG = 2
+X_AT = {(0, 0): 1, (0, 2): 2, (0, 4): 3}
+SHIFT_ON_VECTOR = [(NG - 1, 6), (NG - 1, 7)]
+NORM_ON_VECTOR = [(NG - 1, 7)]
+NORM_PER_STEP = 2
+STORE_TILES = 2
+
+
+def w_transposes_at(j):
+    return [4, 5, 6] if j == 0 else [0, 1, 2]
+
+
+def w_quantises_at(j):
+    return [5, 6, 7] if j == 0 else [2, 3, 4]
+
+
+def tile_rebasedlinearattention_pa_kernel(tc, hidden_states, Wq, Wk, gamma, beta, out_0, out_1):
+    nc = tc.nc
+    x_view = hidden_states.flatten_outer_dims().rearrange("(p i) k -> p i k", i=NT)
+    w_views = [w.rearrange("(a p) k -> p a k", p=P) for w in (Wq, Wk)]
+    o_views = [
+        o.rearrange("b t h d -> (b t) (h d)").rearrange("(p i) c -> p i c", i=NT) for o in (out_0, out_1)
+    ]
+
+    with ExitStack() as ctx:
+        const = ctx.enter_context(tc.tile_pool(name="const", bufs=1))
+        raw = ctx.enter_context(tc.tile_pool(name="raw", bufs=1))
+        stage = ctx.enter_context(tc.tile_pool(name="stage", bufs=3))
+        wq_pool = ctx.enter_context(tc.tile_pool(name="wq", bufs=3))
+        upool = ctx.enter_context(tc.tile_pool(name="u", bufs=3))
+        small = ctx.enter_context(tc.tile_pool(name="small", bufs=3))
+        psum_t = ctx.enter_context(tc.psum_pool(name="psum_t", bufs=3))
+        psum_a = ctx.enter_context(tc.psum_pool(name="psum_a", bufs=5))
+        ctx.enter_context(tc.manual_schedule())
+
+        x_raw = raw.tile([P, NT, K], BF16)
+        w_raw = [
+            raw.tile([P, GROUPS[j][2], K], BF16, name="w_raw", tag="w_raw%d" % GROUPS[j][2], bufs=GROUPS[j][2])
+            for j in range(NG)
+        ]
+
+        def load_x(c):
+            nc.sync.dma_start(out=x_raw[:, 2 * c : 2 * c + 2, :], in_=x_view[:, 2 * c : 2 * c + 2, :])
+
+        def load_w(j):
+            which, h0, nh = GROUPS[j]
+            for a in range(0, nh, 2):
+                nc.sync.dma_start(out=w_raw[j][:, a : a + 2, :], in_=w_views[which][:, h0 + a : h0 + a + 2, :])
+
+        load_w(0)
+        for c in range(NT // 2):
+            load_x(c)
+        for j in range(1, NG):
+            load_w(j)
+
+        ident = const.tile([P, P], F32)
+        make_identity(nc, ident[:])
+        ones = const.tile([P, P], BF16)
+        nc.vector.memset(ones[:], 1.0)
+        gb_row = const.tile([P, 2 * D], BF16)
+        nc.vector.memset(gb_row[:], 0.0)
+        nc.scalar.dma_start(out=gb_row[0:1, 0:D], in_=gamma.unsqueeze(0))
+        nc.scalar.dma_start(out=gb_row[0:1, D : 2 * D], in_=beta.unsqueeze(0))
+
+        x_codes = const.tile([P, PASSES, T], U32, align_bytes=64)
+        x_scales = const.tile([P, PASSES, T], U8, align_bytes=64)
+
+        def transpose_pair(rows, g, dst_words, engine):
+            bank = psum_t.tile([P, 2, 2, P], F32, tag="tp")
+            for l in range(2):
+                words = rows[l].bitcast(F32)
+                for u in range(2):
+                    c0 = (K_PASS // 2) * g + P * u
+                    nc.tensor.transpose(bank[:, l, u, :], words[:, c0 : c0 + P], ident[:])
+            dst = dst_words.rearrange("p (l r u) -> p l r u", l=2, r=P, u=2)
+            src = bank[:].rearrange("p l u r -> p l r u")
+            if engine == "v":
+                nc.vector.tensor_copy(out=dst, in_=src)
+            else:
+                nc.scalar.copy(out=dst, in_=src)
+
+        grouped = {}
+
+        def x_transposes(c, engines):
+            for g in range(PASSES):
+                gr = stage.tile([P, 8 * P], BF16, align_bytes=64, tag="gr2", name="grx")
+                grouped[("x", c, g)] = gr
+                transpose_pair([x_raw[:, 2 * c, :], x_raw[:, 2 * c + 1, :]], g, gr[:].bitcast(F32), engines[g])
+
+        def x_quantises(c):
+            cols = slice(2 * P * c, 2 * P * (c + 1))
+            for g in range(PASSES):
+                nc.vector.quantize_mx(
+                    out=x_codes[:, g, cols].bitcast(FP8X4),
+                    scales=x_scales[:, g, cols],
+                    in_=grouped[("x", c, g)][:],
+                )
+
+        w_codes = {}
+        w_scales = {}
+
+        def w_transposes(j, g, engines):
+            nh = GROUPS[j][2]
+            if g == 0:
+                w_codes[j] = wq_pool.tile([P, PASSES, nh * D], U32, align_bytes=64, tag="w_codes", name="w_codes")
+                w_scales[j] = wq_pool.tile([P, PASSES, nh * D], U8, align_bytes=64, tag="w_scales", name="w_scales")
+            gr = stage.tile([P, 4 * nh * P], BF16, align_bytes=64, tag="gr%d" % nh, name="grw")
+            grouped[("w", j, g)] = gr
+            words = gr[:].bitcast(F32)
+            for a in range(0, nh, 2):
+                transpose_pair(
+                    [w_raw[j][:, a, :], w_raw[j][:, a + 1, :]],
+                    g,
+                    words[:, 2 * P * a : 2 * P * (a + 2)],
+                    engines[(a // 2) % len(engines)],
+                )
+
+        def w_quantise(j, g):
+            nc.vector.quantize_mx(
+                out=w_codes[j][:, g, :].bitcast(FP8X4), scales=w_scales[j][:, g, :], in_=grouped[("w", j, g)][:]
+            )
+
+        for g in range(PASSES):
+            w_transposes(0, g, ["s" if g % 2 == 0 else "v"])
+        for g in range(PASSES):
+            w_quantise(0, g)
+        x_transposes(0, ["v", "s", "v"])
+        x_quantises(0)
+
+        gb_bank = psum_t.tile([P, 2 * D], F32, tag="tp")
+        nc.tensor.matmul(out=gb_bank[:], lhsT=ones[:], rhs=gb_row[:], start=True, stop=True)
+        gb = const.tile([P, 2 * D], F32)
+        nc.scalar.copy(out=gb[:], in_=gb_bank[:])
+
+        seq = [(j, i) for j in range(NG) for i in range(NT)]
+        u_tiles = {}
+        batch_of = {}
+        for j in range(NG):
+            for (i0, i1) in BATCHES[j]:
+                rec = {"j": j, "i0": i0, "i1": i1, "n": (i1 - i0) * GROUPS[j][2]}
+                for i in range(i0, i1):
+                    batch_of[(j, i)] = rec
+
+        def project(j, i):
+            nh = GROUPS[j][2]
+            if i == 0:
+                u_tiles[j] = upool.tile([P, NT, nh * D], F32, tag="u%d" % nh, name="u", bufs=(2 if nh == 2 else 3))
+            acc = psum_a.tile([P, nh * D], F32, tag="acc")
+            toks = slice(P * i, P * (i + 1))
+            for g in range(PASSES):
+                nc.tensor.matmul_mx(
+                    out=acc[:],
+                    lhsT=x_codes[:, g, toks].bitcast(FP8X4),
+                    lhsT_scale=x_scales[:, g, toks],
+                    rhs=w_codes[j][:, g, :].bitcast(FP8X4),
+                    rhs_scale=w_scales[j][:, g, :],
+                    start=(g == 0),
+                    stop=(g == PASSES - 1),
+                )
+            uh = u_tiles[j][:, i, :].rearrange("p (h d) -> p h d", d=D)
+            nc.vector.tensor_tensor(
+                out=uh,
+                in0=acc[:].rearrange("p (h d) -> p h d", d=D),
+                in1=gb[:, 0:D].unsqueeze(1).to_broadcast([P, nh, D]),
+                op=ALU.mult,
+            )
+            shift_engine = nc.vector if (j, i) in SHIFT_ON_VECTOR else nc.gpsimd
+            shift_engine.tensor_tensor(
+                out=uh, in0=uh, in1=gb[:, D : 2 * D].unsqueeze(1).to_broadcast([P, nh, D]), op=ALU.add
+            )
+
+        def statistics(j, i):
+            nh = GROUPS[j][2]
+            rec = batch_of[(j, i)]
+            n = rec["n"]
+            if i == rec["i0"]:
+                rec["st"] = small.tile([P, n, 6], F32, tag="st%d" % n, name="st")
+            st = rec["st"]
+            for h in range(nh):
+                nc.vector.bn_stats(out=st[:, (i - rec["i0"]) * nh + h, :], in_=u_tiles[j][:, i, D * h : D * (h + 1)])
+            if i != rec["i1"] - 1:
+                return None
+            sums = small.tile([P, n, 3], F32, tag="sums%d" % n, name="sums")
+            nc.vector.tensor_reduce(
+                out=sums[:], in_=st[:].rearrange("p n (a c) -> p n c a", a=2), axis=AX.X, op=ALU.add
+            )
+            diff = small.tile([P, n], F32, tag="diff%d" % n, name="diff")
+            nc.vector.tensor_tensor(out=diff[:], in0=st[:, :, 1], in1=st[:, :, 4], op=ALU.subtract)
+            dd = small.tile([P, n], F32, tag="dd%d" % n, name="dd")
+            nc.vector.scalar_tensor_tensor(
+                out=dd[:], in0=diff[:], scalar=float(D // 4), in1=diff[:], op0=ALU.mult, op1=ALU.mult
+            )
+            ssq = small.tile([P, n], F32, tag="ssq%d" % n, name="ssq")
+            nc.vector.scalar_tensor_tensor(
+                out=ssq[:], in0=sums[:, :, 2], scalar=D * LN_EPS, in1=dd[:], op0=ALU.add, op1=ALU.add
+            )
+            sd = small.tile([P, n], F32, tag="sd%d" % n, name="sd")
+            nc.scalar.activation(
+                out=sd[:], in_=ssq[:], func=ACT.Sqrt, scale=(1.0 if GROUPS[j][0] == 0 else 1.0 / D)
+            )
+            rec["sums"] = sums
+            rec["sd"] = sd
+            return rec
+
+        def finish_statistics(rec):
+            n = rec["n"]
+            rs = small.tile([P, n], F32, tag="rs%d" % n, name="rs")
+            nc.vector.reciprocal(out=rs[:], in_=rec["sd"][:])
+            nb = small.tile([P, n], F32, tag="nb%d" % n, name="nb")
+            nc.vector.scalar_tensor_tensor(
+                out=nb[:], in0=rec["sums"][:, :, 1], scalar=-0.5, in1=rs[:], op0=ALU.mult, op1=ALU.mult
+            )
+            rec["rs"] = rs
+            rec["nb"] = nb
+
+        def normalise(j, i):
+            nh = GROUPS[j][2]
+            rec = batch_of[(j, i)]
+            for h in range(nh):
+                col = (i - rec["i0"]) * nh + h
+                piece = u_tiles[j][:, i, D * h : D * (h + 1)]
+                scale = rec["rs"][:, col : col + 1]
+                bias = rec["nb"][:, col : col + 1]
+                if (j, i) in NORM_ON_VECTOR:
+                    nc.vector.tensor_scalar(
+                        out=piece, in0=piece, scalar1=scale, scalar2=bias, op0=ALU.mult, op1=ALU.add
+                    )
+                else:
+                    nc.scalar.activation(out=piece, in_=piece, func=ACT.Identity, scale=scale, bias=bias)
+
+        def store(j, i0, i1):
+            which, h0, nh = GROUPS[j]
+            nc.sync.dma_start(out=o_views[which][:, i0:i1, D * h0 : D * (h0 + nh)], in_=u_tiles[j][:, i0:i1, :])
+
+        pending = None
+        to_normalise = []
+        to_store = []
+        s = 0
+        while s < len(seq) + LAG or pending is not None or to_normalise:
+            if s < len(seq):
+                j, i = seq[s]
+                if (j, i) in X_AT:
+                    x_transposes(X_AT[(j, i)], ["s", "s", "s"])
+                if j + 1 < NG and i in w_transposes_at(j):
+                    w_transposes(j + 1, w_transposes_at(j).index(i), ["s"])
+                project(j, i)
+                if (j, i) in X_AT:
+                    x_quantises(X_AT[(j, i)])
+                if j + 1 < NG and i in w_quantises_at(j):
+                    w_quantise(j + 1, w_quantises_at(j).index(i))
+            if pending is not None:
+                finish_statistics(pending)
+                to_normalise.extend([(pending["j"], i) for i in range(pending["i0"], pending["i1"])])
+                pending = None
+            if LAG <= s < len(seq) + LAG:
+                pending = statistics(*seq[s - LAG])
+            for (j, i) in to_normalise[:NORM_PER_STEP]:
+                normalise(j, i)
+                to_store.append(i)
+                if len(to_store) == STORE_TILES or i == batch_of[(j, i)]["i1"] - 1:
+                    store(j, to_store[0], i + 1)
+                    to_store = []
+            to_normalise = to_normalise[NORM_PER_STEP:]
+            s += 1

@@ -29,7 +29,7 @@ NG = len(GROUPS)
 BATCHES = [[(0, 8)]] * (NG - 1) + [[(0, 4), (4, 6), (6, 8)]]
 LAG = 2
 X_AT = {(0, 0): 1, (0, 2): 2, (0, 4): 3}
-SHIFT_ON_VECTOR = [(NG - 1, 6), (NG - 1, 7)]
+SHIFT_ON_VECTOR = [(j, i) for j in range(NG) for i in range(8)]
 NORM_ON_VECTOR = [(NG - 1, 7)]
 NORM_PER_STEP = 2
 STORE_TILES = 2

@@ -16,31 +16,19 @@ P = 128
 T = 1024
 K = 1536
 D = 128
-H = 12
 NT = T // P
 K_PASS = 512
 PASSES = K // K_PASS
 LN_EPS = 1e-5
+NGROUPS = 6
+NB = 2 * NGROUPS
+N_STATS = 16
 
 FLOPS = 2 * T * (2 * K) * K
 
-GROUPS = [(0, 0, 2), (0, 2, 2), (0, 4, 4), (0, 8, 4), (1, 0, 4), (1, 4, 4), (1, 8, 4)]
-NG = len(GROUPS)
-BATCHES = [[(0, 8)]] * (NG - 1) + [[(0, 4), (4, 6), (6, 8)]]
-LAG = 2
-X_AT = {(0, 0): 1, (0, 2): 2, (0, 4): 3}
-SHIFT_ON_VECTOR = [(j, i) for j in range(NG) for i in range(8)]
-NORM_ON_VECTOR = [(NG - 1, 7)]
-NORM_PER_STEP = 2
-STORE_TILES = 2
-
-
-def w_transposes_at(j):
-    return [4, 5, 6] if j == 0 else [0, 1, 2]
-
-
-def w_quantises_at(j):
-    return [5, 6, 7] if j == 0 else [2, 3, 4]
+PINNED = True
+CHUNKS = ["w0a", "x0", "x1", "w0b", "x2", "x3"] + ["w%d%s" % (j, s) for j in range(1, NGROUPS) for s in "ab"]
+ORDER = [["T","w0a",0],["T","w0a",1],["C","w0a",0],["C","w0a",1],["T","w0a",2],["Q","w0a",0],["T","x0",0],["Q","w0a",1],["C","w0a",2],["C","x0",0],["Q","w0a",2],["T","x0",1],["Q","x0",0],["T","x1",0],["C","x0",1],["C","x1",0],["Q","x0",1],["T","x1",1],["Q","x1",0],["T","w0b",0],["C","x1",1],["C","w0b",0],["Q","x1",1],["T","w0b",1],["Q","w0b",0],["T","x0",2],["C","w0b",1],["C","x0",2],["T","x1",2],["Q","w0b",1],["Q","x0",2],["T","w0b",2],["C","x1",2],["CONST"],["MXN",0,0],["C","w0b",2],["Q","x1",2],["T","x2",0],["Q","w0b",2],["SC",0,0],["T","x3",0],["C","x2",0],["MXT",0,0],["C","x3",0],["SH",0,0],["T","x2",1],["A",0,0],["T","x3",1],["MXT",0,1],["C","x2",1],["Q","x2",0],["Q","x3",0],["C","x3",1],["STN",0,0],["T","x2",2],["A",0,1],["Q","x2",1],["T","x3",2],["Q","x3",1],["UT",0,0],["C","x2",2],["UT",0,1],["C","x3",2],["STT",0,0],["MXN",0,1],["Q","x2",2],["Q","x3",2],["T","w1a",0],["STT",0,1],["T","w1b",0],["C","w1a",0],["SC",0,1],["MXT",1,0],["C","w1b",0],["Q","w1a",0],["T","w1a",1],["SH",0,1],["A",1,0],["T","w1b",1],["MXT",1,1],["C","w1a",1],["Q","w1b",0],["C","w1b",1],["STN",0,1],["T","w1a",2],["A",1,1],["T","w1b",2],["Q","w1a",1],["UT",1,0],["SM",0,"a"],["C","w1a",2],["SM",0,"b"],["Q","w1b",1],["UT",1,1],["SM",0,"c"],["C","w1b",2],["STT",1,0],["MXN",1,0],["SM",0,"d"],["Q","w1a",2],["SM",0,"q"],["Q","w1b",2],["MXN",1,1],["STT",1,1],["SM",0,"e"],["T","w2a",0],["SC",1,0],["T","w2b",0],["SM",0,"f"],["SC",1,1],["C","w2a",0],["SH",1,0],["MXT",2,0],["NMT",0,0],["MXT",2,1],["NMT",0,1],["NMN",0,0],["NMN",0,1],["T","w2a",1],["A",2,0],["STN",1,0],["SH",1,1],["STORE",0],["A",2,1],["UT",2,0],["C","w2b",0],["MXN",2,0],["Q","w2a",0],["STN",1,1],["C","w2a",1],["UT",2,1],["STT",2,0],["MXN",2,1],["SM",1,"a"],["SM",1,"b"],["SC",2,0],["T","w2b",1],["SM",1,"c"],["STT",2,1],["SH",2,0],["T","w2a",2],["C","w2b",1],["SC",2,1],["MXT",3,0],["C","w2a",2],["SM",1,"d"],["Q","w2b",0],["T","w2b",2],["SM",1,"q"],["STN",2,0],["SH",2,1],["A",3,0],["MXT",3,1],["SM",1,"e"],["C","w2b",2],["MXN",3,0],["SM",1,"f"],["A",3,1],["Q","w2a",1],["NMN",1,0],["T","w3a",0],["NMT",1,0],["NMN",1,1],["MXN",3,1],["STN",2,1],["NMT",1,1],["Q","w2b",1],["SM",2,"a"],["UT",3,0],["SM",2,"b"],["Q","w2a",2],["C","w3a",0],["STORE",1],["SM",2,"c"],["UT",3,1],["Q","w2b",2],["T","w3b",0],["SM",2,"d"],["SC",3,0],["SM",2,"q"],["T","w3a",1],["C","w3b",0],["SC",3,1],["SH",3,0],["MXT",4,0],["C","w3a",1],["SM",2,"e"],["STT",3,0],["MXT",4,1],["STT",3,1],["A",4,0],["SH",3,1],["STN",3,0],["T","w3b",1],["A",4,1],["MXN",4,0],["C","w3b",1],["SM",2,"f"],["Q","w3a",0],["NMN",2,0],["NMT",2,0],["MXN",4,1],["NMN",2,1],["STN",3,1],["NMT",2,1],["T","w3a",2],["SC",4,0],["UT",4,0],["C","w3a",2],["T","w3b",2],["SM",3,"a"],["STORE",2],["SM",3,"b"],["SC",4,1],["SH",4,0],["UT",4,1],["C","w3b",2],["MXT",5,0],["STT",4,0],["STT",4,1],["MXT",5,1],["SH",4,1],["A",5,0],["STN",4,0],["T","w4a",0],["A",5,1],["MXN",5,0],["SM",3,"c"],["Q","w3b",0],["C","w4a",0],["SM",3,"d"],["STN",4,1],["SM",3,"q"],["MXN",5,1],["Q","w3a",1],["SM",3,"e"],["SM",4,"a"],["SM",4,"b"],["Q","w3b",1],["T","w4b",0],["SM",3,"f"],["SM",4,"c"],["Q","w3a",2],["T","w4a",1],["NMT",3,0],["NMN",3,0],["NMN",3,1],["NMT",3,1],["SM",4,"d"],["Q","w3b",2],["UT",5,0],["SC",5,0],["SM",4,"q"],["C","w4b",0],["SC",5,1],["STORE",3],["UT",5,1],["SH",5,0],["MXT",6,0],["C","w4a",1],["SM",4,"e"],["STT",5,0],["STT",5,1],["MXT",6,1],["SH",5,1],["A",6,0],["STN",5,0],["T","w4b",1],["A",6,1],["MXN",6,0],["SM",4,"f"],["Q","w4a",0],["C","w4b",1],["NMN",4,0],["NMT",4,0],["MXN",6,1],["NMN",4,1],["STN",5,1],["NMT",4,1],["T","w4a",2],["SC",6,0],["UT",6,0],["C","w4a",2],["SM",5,"a"],["T","w4b",2],["SM",5,"b"],["SC",6,1],["STORE",4],["SH",6,0],["UT",6,1],["C","w4b",2],["STT",6,0],["MXT",7,0],["STT",6,1],["SH",6,1],["MXT",7,1],["STN",6,0],["A",7,0],["T","w5a",0],["A",7,1],["SM",5,"c"],["Q","w4b",0],["MXN",7,0],["SM",5,"d"],["STN",6,1],["C","w5a",0],["SM",5,"q"],["MXN",7,1],["Q","w4a",1],["SM",6,"a"],["SM",5,"e"],["SM",6,"b"],["Q","w4b",1],["T","w5b",0],["SM",5,"f"],["SM",6,"c"],["Q","w4a",2],["NMT",5,0],["T","w5a",1],["NMN",5,0],["NMN",5,1],["NMT",5,1],["SM",6,"d"],["Q","w4b",2],["UT",7,0],["SC",7,0],["SM",6,"q"],["C","w5b",0],["SC",7,1],["STORE",5],["UT",7,1],["SH",7,0],["MXT",8,0],["C","w5a",1],["SM",6,"e"],["STT",7,0],["STT",7,1],["MXT",8,1],["SH",7,1],["A",8,0],["STN",7,0],["T","w5b",1],["A",8,1],["MXN",8,0],["SM",6,"f"],["Q","w5a",0],["C","w5b",1],["NMN",6,0],["NMT",6,0],["MXN",8,1],["NMN",6,1],["STN",7,1],["NMT",6,1],["T","w5a",2],["SC",8,0],["UT",8,0],["C","w5a",2],["SM",7,"a"],["T","w5b",2],["SM",7,"b"],["SC",8,1],["STORE",6],["SH",8,0],["UT",8,1],["C","w5b",2],["STT",8,0],["MXT",9,0],["STT",8,1],["SH",8,1],["MXT",9,1],["STN",8,0],["A",9,0],["A",9,1],["MXN",9,0],["SM",7,"c"],["Q","w5b",0],["SM",7,"d"],["STN",8,1],["SM",7,"q"],["MXN",9,1],["Q","w5a",1],["SM",7,"e"],["SM",8,"a"],["SM",8,"b"],["Q","w5b",1],["SM",7,"f"],["SM",8,"c"],["Q","w5a",2],["NMT",7,0],["NMN",7,0],["NMN",7,1],["NMT",7,1],["SM",8,"d"],["Q","w5b",2],["UT",9,0],["SC",9,0],["SM",8,"q"],["SC",9,1],["STORE",7],["UT",9,1],["SH",9,0],["MXT",10,0],["SM",8,"e"],["STT",9,0],["STT",9,1],["MXT",10,1],["SH",9,1],["A",10,0],["STN",9,0],["A",10,1],["MXN",10,0],["SM",8,"f"],["STN",9,1],["NMT",8,0],["MXN",10,1],["NMN",8,0],["NMT",8,1],["NMN",8,1],["UT",10,0],["SM",9,"a"],["SM",9,"b"],["SC",10,0],["STORE",8],["UT",10,1],["SM",9,"c"],["SC",10,1],["SH",10,0],["MXT",11,0],["STT",10,0],["MXT",11,1],["STT",10,1],["A",11,0],["SH",10,1],["STN",10,0],["A",11,1],["MXN",11,0],["SM",9,"d"],["MXN",11,1],["STN",10,1],["SM",9,"q"],["SM",9,"e"],["SC",11,0],["SM",9,"f"],["SM",10,"a"],["SM",10,"b"],["SH",11,0],["SC",11,1],["NMT",9,0],["NMT",9,1],["UT",11,0],["NMN",9,0],["NMN",9,1],["UT",11,1],["SM",10,"c"],["SH",11,1],["STT",11,0],["STORE",9],["STT",11,1],["STN",11,0],["SM",10,"d"],["STN",11,1],["SM",10,"q"],["SM",10,"e"],["SM",11,"a"],["SM",10,"f"],["SM",11,"b"],["NMN",10,0],["NMT",10,0],["NMN",10,1],["SM",11,"c"],["NMT",10,1],["SM",11,"d"],["SM",11,"q"],["STORE",10],["SM",11,"e"],["SM",11,"f"],["NMN",11,0],["NMT",11,0],["NMN",11,1],["NMT",11,1],["STORE",11]]
 
 
 def tile_rebasedlinearattention_pa_kernel(tc, hidden_states, Wq, Wk, gamma, beta, out_0, out_1):
@@ -53,241 +41,279 @@ def tile_rebasedlinearattention_pa_kernel(tc, hidden_states, Wq, Wk, gamma, beta
 
     with ExitStack() as ctx:
         const = ctx.enter_context(tc.tile_pool(name="const", bufs=1))
-        raw = ctx.enter_context(tc.tile_pool(name="raw", bufs=1))
-        stage = ctx.enter_context(tc.tile_pool(name="stage", bufs=3))
+        raw = ctx.enter_context(tc.tile_pool(name="raw", bufs=8))
+        stage = ctx.enter_context(tc.tile_pool(name="stage", bufs=8))
         wq_pool = ctx.enter_context(tc.tile_pool(name="wq", bufs=3))
-        upool = ctx.enter_context(tc.tile_pool(name="u", bufs=3))
+        ut_pool = ctx.enter_context(tc.tile_pool(name="ut", bufs=4))
+        opool = ctx.enter_context(tc.tile_pool(name="o", bufs=5))
         small = ctx.enter_context(tc.tile_pool(name="small", bufs=3))
-        psum_t = ctx.enter_context(tc.psum_pool(name="psum_t", bufs=3))
-        psum_a = ctx.enter_context(tc.psum_pool(name="psum_a", bufs=5))
-        ctx.enter_context(tc.manual_schedule())
+        psum_t = ctx.enter_context(tc.psum_pool(name="psum_t", bufs=2))
+        psum_a = ctx.enter_context(tc.psum_pool(name="psum_a", bufs=2))
+        psum_u = ctx.enter_context(tc.psum_pool(name="psum_u", bufs=4))
+        if PINNED:
+            ctx.enter_context(tc.manual_schedule())
 
-        x_raw = raw.tile([P, NT, K], BF16)
-        w_raw = [
-            raw.tile([P, GROUPS[j][2], K], BF16, name="w_raw", tag="w_raw%d" % GROUPS[j][2], bufs=GROUPS[j][2])
-            for j in range(NG)
-        ]
+        x_raw = const.tile([P, NT, K], BF16)
+        x_codes = const.tile([P, PASSES, T], U32, align_bytes=64)
+        x_scales = const.tile([P, PASSES, T], U8, align_bytes=64)
+        tiles = {}
 
-        def load_x(c):
-            nc.sync.dma_start(out=x_raw[:, 2 * c : 2 * c + 2, :], in_=x_view[:, 2 * c : 2 * c + 2, :])
+        def rows_of(chunk):
+            if chunk[0] == "x":
+                c = int(chunk[1:])
+                return [x_raw[:, 2 * c, :], x_raw[:, 2 * c + 1, :]]
+            return [tiles[("raw", chunk)][:, 0, :], tiles[("raw", chunk)][:, 1, :]]
 
-        def load_w(j):
-            which, h0, nh = GROUPS[j]
-            for a in range(0, nh, 2):
-                nc.sync.dma_start(out=w_raw[j][:, a : a + 2, :], in_=w_views[which][:, h0 + a : h0 + a + 2, :])
+        def load(chunk):
+            if chunk[0] == "x":
+                c = int(chunk[1:])
+                nc.sync.dma_start(out=x_raw[:, 2 * c : 2 * c + 2, :], in_=x_view[:, 2 * c : 2 * c + 2, :])
+            else:
+                j = int(chunk[1:-1])
+                h0 = 4 * (j % 3) + (0 if chunk[-1] == "a" else 2)
+                t = raw.tile([P, 2, K], BF16, name="w_raw", tag="w_raw")
+                tiles[("raw", chunk)] = t
+                nc.sync.dma_start(out=t[:], in_=w_views[j // 3][:, h0 : h0 + 2, :])
 
-        load_w(0)
-        for c in range(NT // 2):
-            load_x(c)
-        for j in range(1, NG):
-            load_w(j)
+        def prep_t(chunk, g):
+            bank = psum_t.tile([P, 2, 2, P], F32, tag="tp", name="tp")
+            tiles[("tp", chunk, g)] = bank
+            rows = rows_of(chunk)
+            for l in range(2):
+                words = rows[l].bitcast(F32)
+                for u in range(2):
+                    c0 = (K_PASS // 2) * g + P * u
+                    nc.tensor.transpose(bank[:, l, u, :], words[:, c0 : c0 + P], ident[:])
 
+        def prep_c(chunk, g):
+            gr = stage.tile([P, 8 * P], BF16, align_bytes=64, tag="gr", name="gr")
+            tiles[("gr", chunk, g)] = gr
+            dst = gr[:].bitcast(F32).rearrange("p (l r u) -> p l r u", l=2, r=P, u=2)
+            src = tiles[("tp", chunk, g)][:].rearrange("p l u r -> p l r u")
+            if CHUNKS.index(chunk) < 4 and g % 2 == 1:
+                nc.vector.tensor_copy(out=dst, in_=src)
+            else:
+                nc.scalar.copy(out=dst, in_=src)
+
+        def prep_q(chunk, g):
+            if chunk[0] == "x":
+                c = int(chunk[1:])
+                cols = slice(2 * P * c, 2 * P * (c + 1))
+                codes, scales = x_codes, x_scales
+            else:
+                j = int(chunk[1:-1])
+                if ("wc", j) not in tiles:
+                    tiles[("wc", j)] = wq_pool.tile([P, PASSES, 4 * D], U32, align_bytes=64, tag="wc", name="wc")
+                    tiles[("ws", j)] = wq_pool.tile([P, PASSES, 4 * D], U8, align_bytes=64, tag="ws", name="ws")
+                codes, scales = tiles[("wc", j)], tiles[("ws", j)]
+                cols = slice(0, 2 * D) if chunk[-1] == "a" else slice(2 * D, 4 * D)
+            nc.vector.quantize_mx(
+                out=codes[:, g, cols].bitcast(FP8X4), scales=scales[:, g, cols], in_=tiles[("gr", chunk, g)][:]
+            )
+
+        def o_tile(b):
+            if ("o", b) not in tiles:
+                tiles[("o", b)] = opool.tile([P, 4, 4 * D], F32, tag="o", name="o")
+            return tiles[("o", b)]
+
+        def st_tile(b):
+            if ("st", b) not in tiles:
+                tiles[("st", b)] = small.tile([P, N_STATS, 6], F32, tag="st", name="st")
+            return tiles[("st", b)]
+
+        def mxn(b, u):
+            j, th = b // 2, b % 2
+            acc = psum_a.tile([P, 2, 2 * D], F32, tag="acc", name="acc")
+            tiles[("accn", b, u)] = acc
+            for t2 in range(2):
+                i = 4 * th + 2 * u + t2
+                toks = slice(P * i, P * (i + 1))
+                for g in range(PASSES):
+                    nc.tensor.matmul_mx(
+                        out=acc[:, t2, :],
+                        lhsT=x_codes[:, g, toks].bitcast(FP8X4),
+                        lhsT_scale=x_scales[:, g, toks],
+                        rhs=tiles[("wc", j)][:, g, 0 : 2 * D].bitcast(FP8X4),
+                        rhs_scale=tiles[("ws", j)][:, g, 0 : 2 * D],
+                        start=(g == 0),
+                        stop=(g == PASSES - 1),
+                    )
+
+        def n_view(b, u):
+            return o_tile(b)[:, 2 * u : 2 * u + 2, 0 : 2 * D].rearrange("p t (h d) -> p t h d", d=D)
+
+        def sc(b, u):
+            nc.vector.tensor_tensor(
+                out=n_view(b, u),
+                in0=tiles[("accn", b, u)][:].rearrange("p t (h d) -> p t h d", d=D),
+                in1=gb[:, 0:D].unsqueeze(1).unsqueeze(1).to_broadcast([P, 2, 2, D]),
+                op=ALU.mult,
+            )
+
+        def sh(b, u):
+            nc.gpsimd.tensor_tensor(
+                out=n_view(b, u),
+                in0=n_view(b, u),
+                in1=gb[:, D : 2 * D].unsqueeze(1).unsqueeze(1).to_broadcast([P, 2, 2, D]),
+                op=ALU.add,
+            )
+
+        def stn(b, u):
+            for t2 in range(2):
+                for h in range(2):
+                    nc.vector.bn_stats(
+                        out=st_tile(b)[:, 4 * u + 2 * t2 + h, :], in_=o_tile(b)[:, 2 * u + t2, D * h : D * (h + 1)]
+                    )
+
+        def mxt(b, u):
+            j, th = b // 2, b % 2
+            acc = psum_a.tile([P, 4 * P], F32, tag="acc", name="acc")
+            tiles[("acct", b, u)] = acc
+            feats = slice(D * (2 + u), D * (3 + u))
+            toks = slice(4 * P * th, 4 * P * (th + 1))
+            for g in range(PASSES):
+                nc.tensor.matmul_mx(
+                    out=acc[:],
+                    lhsT=tiles[("wc", j)][:, g, feats].bitcast(FP8X4),
+                    lhsT_scale=tiles[("ws", j)][:, g, feats],
+                    rhs=x_codes[:, g, toks].bitcast(FP8X4),
+                    rhs_scale=x_scales[:, g, toks],
+                    start=(g == 0),
+                    stop=(g == PASSES - 1),
+                )
+
+        def affine_t(b, u):
+            ut = ut_pool.tile([P, 4 * P], F32, tag="ut", name="ut")
+            tiles[("ut", b, u)] = ut
+            nc.scalar.activation(
+                out=ut[:], in_=tiles[("acct", b, u)][:], func=ACT.Identity, scale=gcol[:, 0:1], bias=gcol[:, 1:2]
+            )
+
+        def ut_back(b, u):
+            bank = psum_u.tile([P, 4, D], F32, tag="U", name="U")
+            tiles[("U", b, u)] = bank
+            for t in range(4):
+                nc.tensor.transpose(bank[:, t, :], tiles[("ut", b, u)][:, P * t : P * (t + 1)], ident[:])
+
+        def stt(b, u):
+            for t in range(4):
+                nc.vector.bn_stats(out=st_tile(b)[:, 8 + 4 * u + t, :], in_=tiles[("U", b, u)][:, t, :])
+
+        def sm(b, k):
+            n = N_STATS
+            st = st_tile(b)
+            if k == "a":
+                tiles[("sums", b)] = small.tile([P, n, 3], F32, tag="sums", name="sums")
+                nc.vector.tensor_reduce(
+                    out=tiles[("sums", b)][:], in_=st[:].rearrange("p n (a c) -> p n c a", a=2), axis=AX.X, op=ALU.add
+                )
+            elif k == "b":
+                tiles[("diff", b)] = small.tile([P, n], F32, tag="diff", name="diff")
+                nc.vector.tensor_tensor(out=tiles[("diff", b)][:], in0=st[:, :, 1], in1=st[:, :, 4], op=ALU.subtract)
+            elif k == "c":
+                tiles[("dd", b)] = small.tile([P, n], F32, tag="dd", name="dd")
+                nc.vector.scalar_tensor_tensor(
+                    out=tiles[("dd", b)][:],
+                    in0=tiles[("diff", b)][:],
+                    scalar=float(D // 4),
+                    in1=tiles[("diff", b)][:],
+                    op0=ALU.mult,
+                    op1=ALU.mult,
+                )
+            elif k == "d":
+                tiles[("ssq", b)] = small.tile([P, n], F32, tag="ssq", name="ssq")
+                nc.vector.scalar_tensor_tensor(
+                    out=tiles[("ssq", b)][:],
+                    in0=tiles[("sums", b)][:, :, 2],
+                    scalar=D * LN_EPS,
+                    in1=tiles[("dd", b)][:],
+                    op0=ALU.add,
+                    op1=ALU.add,
+                )
+            elif k == "q":
+                tiles[("sd", b)] = small.tile([P, n], F32, tag="sd", name="sd")
+                nc.scalar.activation(
+                    out=tiles[("sd", b)][:],
+                    in_=tiles[("ssq", b)][:],
+                    func=ACT.Sqrt,
+                    scale=(1.0 if b // 2 < 3 else 1.0 / D),
+                )
+            elif k == "e":
+                tiles[("rs", b)] = small.tile([P, n], F32, tag="rs", name="rs")
+                nc.vector.reciprocal(out=tiles[("rs", b)][:], in_=tiles[("sd", b)][:])
+            else:
+                tiles[("nb", b)] = small.tile([P, n], F32, tag="nb", name="nb")
+                nc.vector.scalar_tensor_tensor(
+                    out=tiles[("nb", b)][:],
+                    in0=tiles[("sums", b)][:, :, 1],
+                    scalar=-0.5,
+                    in1=tiles[("rs", b)][:],
+                    op0=ALU.mult,
+                    op1=ALU.mult,
+                )
+
+        def norm(engine, dst, src, b, col):
+            scale = tiles[("rs", b)][:, col : col + 1]
+            bias = tiles[("nb", b)][:, col : col + 1]
+            if engine == "v":
+                nc.vector.tensor_scalar(out=dst, in0=src, scalar1=scale, scalar2=bias, op0=ALU.mult, op1=ALU.add)
+            else:
+                nc.scalar.activation(out=dst, in_=src, func=ACT.Identity, scale=scale, bias=bias)
+
+        def nmn(b, u):
+            for t2 in range(2):
+                for h in range(2):
+                    piece = o_tile(b)[:, 2 * u + t2, D * h : D * (h + 1)]
+                    norm("v", piece, piece, b, 4 * u + 2 * t2 + h)
+
+        def nmt(b, u):
+            for t in range(4):
+                norm("s", o_tile(b)[:, t, D * (2 + u) : D * (3 + u)], tiles[("U", b, u)][:, t, :], b, 8 + 4 * u + t)
+
+        def store(b):
+            j, th = b // 2, b % 2
+            cols = slice(4 * D * (j % 3), 4 * D * (j % 3 + 1))
+            nc.sync.dma_start(out=o_views[j // 3][:, 4 * th : 4 * th + 4, cols], in_=o_tile(b)[:])
+
+        for chunk in CHUNKS:
+            load(chunk)
         ident = const.tile([P, P], F32)
         make_identity(nc, ident[:])
         ones = const.tile([P, P], BF16)
         nc.vector.memset(ones[:], 1.0)
         gb_row = const.tile([P, 2 * D], BF16)
         nc.vector.memset(gb_row[:], 0.0)
+        warm = const.tile([P, 1], F32)
+        nc.vector.memset(warm[:], 1.0)
         nc.scalar.dma_start(out=gb_row[0:1, 0:D], in_=gamma.unsqueeze(0))
         nc.scalar.dma_start(out=gb_row[0:1, D : 2 * D], in_=beta.unsqueeze(0))
-
-        x_codes = const.tile([P, PASSES, T], U32, align_bytes=64)
-        x_scales = const.tile([P, PASSES, T], U8, align_bytes=64)
-
-        def transpose_pair(rows, g, dst_words, engine):
-            bank = psum_t.tile([P, 2, 2, P], F32, tag="tp")
-            for l in range(2):
-                words = rows[l].bitcast(F32)
-                for u in range(2):
-                    c0 = (K_PASS // 2) * g + P * u
-                    nc.tensor.transpose(bank[:, l, u, :], words[:, c0 : c0 + P], ident[:])
-            dst = dst_words.rearrange("p (l r u) -> p l r u", l=2, r=P, u=2)
-            src = bank[:].rearrange("p l u r -> p l r u")
-            if engine == "v":
-                nc.vector.tensor_copy(out=dst, in_=src)
-            else:
-                nc.scalar.copy(out=dst, in_=src)
-
-        grouped = {}
-
-        def x_transposes(c, engines):
-            for g in range(PASSES):
-                gr = stage.tile([P, 8 * P], BF16, align_bytes=64, tag="gr2", name="grx")
-                grouped[("x", c, g)] = gr
-                transpose_pair([x_raw[:, 2 * c, :], x_raw[:, 2 * c + 1, :]], g, gr[:].bitcast(F32), engines[g])
-
-        def x_quantises(c):
-            cols = slice(2 * P * c, 2 * P * (c + 1))
-            for g in range(PASSES):
-                nc.vector.quantize_mx(
-                    out=x_codes[:, g, cols].bitcast(FP8X4),
-                    scales=x_scales[:, g, cols],
-                    in_=grouped[("x", c, g)][:],
-                )
-
-        w_codes = {}
-        w_scales = {}
-
-        def w_transposes(j, g, engines):
-            nh = GROUPS[j][2]
-            if g == 0:
-                w_codes[j] = wq_pool.tile([P, PASSES, nh * D], U32, align_bytes=64, tag="w_codes", name="w_codes")
-                w_scales[j] = wq_pool.tile([P, PASSES, nh * D], U8, align_bytes=64, tag="w_scales", name="w_scales")
-            gr = stage.tile([P, 4 * nh * P], BF16, align_bytes=64, tag="gr%d" % nh, name="grw")
-            grouped[("w", j, g)] = gr
-            words = gr[:].bitcast(F32)
-            for a in range(0, nh, 2):
-                transpose_pair(
-                    [w_raw[j][:, a, :], w_raw[j][:, a + 1, :]],
-                    g,
-                    words[:, 2 * P * a : 2 * P * (a + 2)],
-                    engines[(a // 2) % len(engines)],
-                )
-
-        def w_quantise(j, g):
-            nc.vector.quantize_mx(
-                out=w_codes[j][:, g, :].bitcast(FP8X4), scales=w_scales[j][:, g, :], in_=grouped[("w", j, g)][:]
-            )
-
-        for g in range(PASSES):
-            w_transposes(0, g, ["s" if g % 2 == 0 else "v"])
-        for g in range(PASSES):
-            w_quantise(0, g)
-        x_transposes(0, ["v", "s", "v"])
-        x_quantises(0)
-
-        gb_bank = psum_t.tile([P, 2 * D], F32, tag="tp")
-        nc.tensor.matmul(out=gb_bank[:], lhsT=ones[:], rhs=gb_row[:], start=True, stop=True)
+        nc.scalar.activation(out=warm[:], in_=warm[:], func=ACT.Sqrt)
         gb = const.tile([P, 2 * D], F32)
-        nc.scalar.copy(out=gb[:], in_=gb_bank[:])
+        gcol = const.tile([P, 2], F32)
 
-        seq = [(j, i) for j in range(NG) for i in range(NT)]
-        u_tiles = {}
-        batch_of = {}
-        for j in range(NG):
-            for (i0, i1) in BATCHES[j]:
-                rec = {"j": j, "i0": i0, "i1": i1, "n": (i1 - i0) * GROUPS[j][2]}
-                for i in range(i0, i1):
-                    batch_of[(j, i)] = rec
-
-        def project(j, i):
-            nh = GROUPS[j][2]
-            if i == 0:
-                u_tiles[j] = upool.tile([P, NT, nh * D], F32, tag="u%d" % nh, name="u", bufs=(2 if nh == 2 else 3))
-            acc = psum_a.tile([P, nh * D], F32, tag="acc")
-            toks = slice(P * i, P * (i + 1))
-            for g in range(PASSES):
-                nc.tensor.matmul_mx(
-                    out=acc[:],
-                    lhsT=x_codes[:, g, toks].bitcast(FP8X4),
-                    lhsT_scale=x_scales[:, g, toks],
-                    rhs=w_codes[j][:, g, :].bitcast(FP8X4),
-                    rhs_scale=w_scales[j][:, g, :],
-                    start=(g == 0),
-                    stop=(g == PASSES - 1),
+        def constants():
+            gb_bank = psum_u.tile([P, 2 * D], F32, tag="U", name="gb_bank")
+            nc.tensor.matmul(out=gb_bank[:], lhsT=ones[:], rhs=gb_row[:], start=True, stop=True)
+            nc.scalar.copy(out=gb[:], in_=gb_bank[:])
+            col_bank = psum_u.tile([P, 2, 64], F32, tag="U", name="col_bank")
+            for k in range(2):
+                nc.tensor.matmul(
+                    out=col_bank[:, k, :], lhsT=gb_row[:, D * k : D * (k + 1)], rhs=ones[:, 0:64], start=True, stop=True
                 )
-            uh = u_tiles[j][:, i, :].rearrange("p (h d) -> p h d", d=D)
-            nc.vector.tensor_tensor(
-                out=uh,
-                in0=acc[:].rearrange("p (h d) -> p h d", d=D),
-                in1=gb[:, 0:D].unsqueeze(1).to_broadcast([P, nh, D]),
-                op=ALU.mult,
-            )
-            shift_engine = nc.vector if (j, i) in SHIFT_ON_VECTOR else nc.gpsimd
-            shift_engine.tensor_tensor(
-                out=uh, in0=uh, in1=gb[:, D : 2 * D].unsqueeze(1).to_broadcast([P, nh, D]), op=ALU.add
-            )
+            nc.scalar.copy(out=gcol[:], in_=col_bank[:, :, 0])
 
-        def statistics(j, i):
-            nh = GROUPS[j][2]
-            rec = batch_of[(j, i)]
-            n = rec["n"]
-            if i == rec["i0"]:
-                rec["st"] = small.tile([P, n, 6], F32, tag="st%d" % n, name="st")
-            st = rec["st"]
-            for h in range(nh):
-                nc.vector.bn_stats(out=st[:, (i - rec["i0"]) * nh + h, :], in_=u_tiles[j][:, i, D * h : D * (h + 1)])
-            if i != rec["i1"] - 1:
-                return None
-            sums = small.tile([P, n, 3], F32, tag="sums%d" % n, name="sums")
-            nc.vector.tensor_reduce(
-                out=sums[:], in_=st[:].rearrange("p n (a c) -> p n c a", a=2), axis=AX.X, op=ALU.add
-            )
-            diff = small.tile([P, n], F32, tag="diff%d" % n, name="diff")
-            nc.vector.tensor_tensor(out=diff[:], in0=st[:, :, 1], in1=st[:, :, 4], op=ALU.subtract)
-            dd = small.tile([P, n], F32, tag="dd%d" % n, name="dd")
-            nc.vector.scalar_tensor_tensor(
-                out=dd[:], in0=diff[:], scalar=float(D // 4), in1=diff[:], op0=ALU.mult, op1=ALU.mult
-            )
-            ssq = small.tile([P, n], F32, tag="ssq%d" % n, name="ssq")
-            nc.vector.scalar_tensor_tensor(
-                out=ssq[:], in0=sums[:, :, 2], scalar=D * LN_EPS, in1=dd[:], op0=ALU.add, op1=ALU.add
-            )
-            sd = small.tile([P, n], F32, tag="sd%d" % n, name="sd")
-            nc.scalar.activation(
-                out=sd[:], in_=ssq[:], func=ACT.Sqrt, scale=(1.0 if GROUPS[j][0] == 0 else 1.0 / D)
-            )
-            rec["sums"] = sums
-            rec["sd"] = sd
-            return rec
-
-        def finish_statistics(rec):
-            n = rec["n"]
-            rs = small.tile([P, n], F32, tag="rs%d" % n, name="rs")
-            nc.vector.reciprocal(out=rs[:], in_=rec["sd"][:])
-            nb = small.tile([P, n], F32, tag="nb%d" % n, name="nb")
-            nc.vector.scalar_tensor_tensor(
-                out=nb[:], in0=rec["sums"][:, :, 1], scalar=-0.5, in1=rs[:], op0=ALU.mult, op1=ALU.mult
-            )
-            rec["rs"] = rs
-            rec["nb"] = nb
-
-        def normalise(j, i):
-            nh = GROUPS[j][2]
-            rec = batch_of[(j, i)]
-            for h in range(nh):
-                col = (i - rec["i0"]) * nh + h
-                piece = u_tiles[j][:, i, D * h : D * (h + 1)]
-                scale = rec["rs"][:, col : col + 1]
-                bias = rec["nb"][:, col : col + 1]
-                if (j, i) in NORM_ON_VECTOR:
-                    nc.vector.tensor_scalar(
-                        out=piece, in0=piece, scalar1=scale, scalar2=bias, op0=ALU.mult, op1=ALU.add
-                    )
-                else:
-                    nc.scalar.activation(out=piece, in_=piece, func=ACT.Identity, scale=scale, bias=bias)
-
-        def store(j, i0, i1):
-            which, h0, nh = GROUPS[j]
-            nc.sync.dma_start(out=o_views[which][:, i0:i1, D * h0 : D * (h0 + nh)], in_=u_tiles[j][:, i0:i1, :])
-
-        pending = None
-        to_normalise = []
-        to_store = []
-        s = 0
-        while s < len(seq) + LAG or pending is not None or to_normalise:
-            if s < len(seq):
-                j, i = seq[s]
-                if (j, i) in X_AT:
-                    x_transposes(X_AT[(j, i)], ["s", "s", "s"])
-                if j + 1 < NG and i in w_transposes_at(j):
-                    w_transposes(j + 1, w_transposes_at(j).index(i), ["s"])
-                project(j, i)
-                if (j, i) in X_AT:
-                    x_quantises(X_AT[(j, i)])
-                if j + 1 < NG and i in w_quantises_at(j):
-                    w_quantise(j + 1, w_quantises_at(j).index(i))
-            if pending is not None:
-                finish_statistics(pending)
-                to_normalise.extend([(pending["j"], i) for i in range(pending["i0"], pending["i1"])])
-                pending = None
-            if LAG <= s < len(seq) + LAG:
-                pending = statistics(*seq[s - LAG])
-            for (j, i) in to_normalise[:NORM_PER_STEP]:
-                normalise(j, i)
-                to_store.append(i)
-                if len(to_store) == STORE_TILES or i == batch_of[(j, i)]["i1"] - 1:
-                    store(j, to_store[0], i + 1)
-                    to_store = []
-            to_normalise = to_normalise[NORM_PER_STEP:]
-            s += 1
+        kinds = {
+            "T": prep_t, "C": prep_c, "Q": prep_q,
+            "MXN": mxn, "SC": sc, "SH": sh, "STN": stn, "MXT": mxt, "A": affine_t, "UT": ut_back, "STT": stt,
+            "NMN": nmn, "NMT": nmt,
+        }
+        for entry in ORDER:
+            kind = entry[0]
+            if kind == "CONST":
+                constants()
+            elif kind == "SM":
+                sm(entry[1], entry[2])
+            elif kind == "STORE":
+                store(entry[1])
+            else:
+                kinds[kind](entry[1], entry[2])

@@ -28,7 +28,7 @@ FLOPS = 2 * T * (2 * K) * K
 
 PINNED = True
 CHUNKS = ["w0a", "x0", "x1", "w0b", "x2", "x3"] + ["w%d%s" % (j, s) for j in range(1, NGROUPS) for s in "ab"]
-ORDER = [["T","w0a",0],["T","w0a",1],["C","w0a",0],["C","w0a",1],["T","w0a",2],["Q","w0a",0],["T","x0",0],["Q","w0a",1],["C","w0a",2],["C","x0",0],["Q","w0a",2],["T","x0",1],["Q","x0",0],["T","x1",0],["C","x0",1],["C","x1",0],["Q","x0",1],["T","x1",1],["Q","x1",0],["T","w0b",0],["C","x1",1],["C","w0b",0],["Q","x1",1],["T","w0b",1],["Q","w0b",0],["T","x0",2],["C","w0b",1],["C","x0",2],["T","x1",2],["Q","w0b",1],["Q","x0",2],["T","w0b",2],["C","x1",2],["CONST"],["MXN",0,0],["C","w0b",2],["Q","x1",2],["T","x2",0],["Q","w0b",2],["SC",0,0],["T","x3",0],["C","x2",0],["MXT",0,0],["C","x3",0],["SH",0,0],["T","x2",1],["A",0,0],["T","x3",1],["MXT",0,1],["C","x2",1],["Q","x2",0],["Q","x3",0],["C","x3",1],["STN",0,0],["T","x2",2],["A",0,1],["Q","x2",1],["T","x3",2],["Q","x3",1],["UT",0,0],["C","x2",2],["UT",0,1],["C","x3",2],["STT",0,0],["MXN",0,1],["Q","x2",2],["Q","x3",2],["T","w1a",0],["STT",0,1],["T","w1b",0],["C","w1a",0],["SC",0,1],["MXT",1,0],["C","w1b",0],["Q","w1a",0],["T","w1a",1],["SH",0,1],["A",1,0],["T","w1b",1],["MXT",1,1],["C","w1a",1],["Q","w1b",0],["C","w1b",1],["STN",0,1],["T","w1a",2],["A",1,1],["T","w1b",2],["Q","w1a",1],["UT",1,0],["SM",0,"a"],["C","w1a",2],["SM",0,"b"],["Q","w1b",1],["UT",1,1],["SM",0,"c"],["C","w1b",2],["STT",1,0],["MXN",1,0],["SM",0,"d"],["Q","w1a",2],["SM",0,"q"],["Q","w1b",2],["MXN",1,1],["STT",1,1],["SM",0,"e"],["T","w2a",0],["SC",1,0],["T","w2b",0],["SM",0,"f"],["SC",1,1],["C","w2a",0],["SH",1,0],["MXT",2,0],["NMT",0,0],["MXT",2,1],["NMT",0,1],["NMN",0,0],["NMN",0,1],["T","w2a",1],["A",2,0],["STN",1,0],["SH",1,1],["STORE",0],["A",2,1],["UT",2,0],["C","w2b",0],["MXN",2,0],["Q","w2a",0],["STN",1,1],["C","w2a",1],["UT",2,1],["STT",2,0],["MXN",2,1],["SM",1,"a"],["SM",1,"b"],["SC",2,0],["T","w2b",1],["SM",1,"c"],["STT",2,1],["SH",2,0],["T","w2a",2],["C","w2b",1],["SC",2,1],["MXT",3,0],["C","w2a",2],["SM",1,"d"],["Q","w2b",0],["T","w2b",2],["SM",1,"q"],["STN",2,0],["SH",2,1],["A",3,0],["MXT",3,1],["SM",1,"e"],["C","w2b",2],["MXN",3,0],["SM",1,"f"],["A",3,1],["Q","w2a",1],["NMN",1,0],["T","w3a",0],["NMT",1,0],["NMN",1,1],["MXN",3,1],["STN",2,1],["NMT",1,1],["Q","w2b",1],["SM",2,"a"],["UT",3,0],["SM",2,"b"],["Q","w2a",2],["C","w3a",0],["STORE",1],["SM",2,"c"],["UT",3,1],["Q","w2b",2],["T","w3b",0],["SM",2,"d"],["SC",3,0],["SM",2,"q"],["T","w3a",1],["C","w3b",0],["SC",3,1],["SH",3,0],["MXT",4,0],["C","w3a",1],["SM",2,"e"],["STT",3,0],["MXT",4,1],["STT",3,1],["A",4,0],["SH",3,1],["STN",3,0],["T","w3b",1],["A",4,1],["MXN",4,0],["C","w3b",1],["SM",2,"f"],["Q","w3a",0],["NMN",2,0],["NMT",2,0],["MXN",4,1],["NMN",2,1],["STN",3,1],["NMT",2,1],["T","w3a",2],["SC",4,0],["UT",4,0],["C","w3a",2],["T","w3b",2],["SM",3,"a"],["STORE",2],["SM",3,"b"],["SC",4,1],["SH",4,0],["UT",4,1],["C","w3b",2],["MXT",5,0],["STT",4,0],["STT",4,1],["MXT",5,1],["SH",4,1],["A",5,0],["STN",4,0],["T","w4a",0],["A",5,1],["MXN",5,0],["SM",3,"c"],["Q","w3b",0],["C","w4a",0],["SM",3,"d"],["STN",4,1],["SM",3,"q"],["MXN",5,1],["Q","w3a",1],["SM",3,"e"],["SM",4,"a"],["SM",4,"b"],["Q","w3b",1],["T","w4b",0],["SM",3,"f"],["SM",4,"c"],["Q","w3a",2],["T","w4a",1],["NMT",3,0],["NMN",3,0],["NMN",3,1],["NMT",3,1],["SM",4,"d"],["Q","w3b",2],["UT",5,0],["SC",5,0],["SM",4,"q"],["C","w4b",0],["SC",5,1],["STORE",3],["UT",5,1],["SH",5,0],["MXT",6,0],["C","w4a",1],["SM",4,"e"],["STT",5,0],["STT",5,1],["MXT",6,1],["SH",5,1],["A",6,0],["STN",5,0],["T","w4b",1],["A",6,1],["MXN",6,0],["SM",4,"f"],["Q","w4a",0],["C","w4b",1],["NMN",4,0],["NMT",4,0],["MXN",6,1],["NMN",4,1],["STN",5,1],["NMT",4,1],["T","w4a",2],["SC",6,0],["UT",6,0],["C","w4a",2],["SM",5,"a"],["T","w4b",2],["SM",5,"b"],["SC",6,1],["STORE",4],["SH",6,0],["UT",6,1],["C","w4b",2],["STT",6,0],["MXT",7,0],["STT",6,1],["SH",6,1],["MXT",7,1],["STN",6,0],["A",7,0],["T","w5a",0],["A",7,1],["SM",5,"c"],["Q","w4b",0],["MXN",7,0],["SM",5,"d"],["STN",6,1],["C","w5a",0],["SM",5,"q"],["MXN",7,1],["Q","w4a",1],["SM",6,"a"],["SM",5,"e"],["SM",6,"b"],["Q","w4b",1],["T","w5b",0],["SM",5,"f"],["SM",6,"c"],["Q","w4a",2],["NMT",5,0],["T","w5a",1],["NMN",5,0],["NMN",5,1],["NMT",5,1],["SM",6,"d"],["Q","w4b",2],["UT",7,0],["SC",7,0],["SM",6,"q"],["C","w5b",0],["SC",7,1],["STORE",5],["UT",7,1],["SH",7,0],["MXT",8,0],["C","w5a",1],["SM",6,"e"],["STT",7,0],["STT",7,1],["MXT",8,1],["SH",7,1],["A",8,0],["STN",7,0],["T","w5b",1],["A",8,1],["MXN",8,0],["SM",6,"f"],["Q","w5a",0],["C","w5b",1],["NMN",6,0],["NMT",6,0],["MXN",8,1],["NMN",6,1],["STN",7,1],["NMT",6,1],["T","w5a",2],["SC",8,0],["UT",8,0],["C","w5a",2],["SM",7,"a"],["T","w5b",2],["SM",7,"b"],["SC",8,1],["STORE",6],["SH",8,0],["UT",8,1],["C","w5b",2],["STT",8,0],["MXT",9,0],["STT",8,1],["SH",8,1],["MXT",9,1],["STN",8,0],["A",9,0],["A",9,1],["MXN",9,0],["SM",7,"c"],["Q","w5b",0],["SM",7,"d"],["STN",8,1],["SM",7,"q"],["MXN",9,1],["Q","w5a",1],["SM",7,"e"],["SM",8,"a"],["SM",8,"b"],["Q","w5b",1],["SM",7,"f"],["SM",8,"c"],["Q","w5a",2],["NMT",7,0],["NMN",7,0],["NMN",7,1],["NMT",7,1],["SM",8,"d"],["Q","w5b",2],["UT",9,0],["SC",9,0],["SM",8,"q"],["SC",9,1],["STORE",7],["UT",9,1],["SH",9,0],["MXT",10,0],["SM",8,"e"],["STT",9,0],["STT",9,1],["MXT",10,1],["SH",9,1],["A",10,0],["STN",9,0],["A",10,1],["MXN",10,0],["SM",8,"f"],["STN",9,1],["NMT",8,0],["MXN",10,1],["NMN",8,0],["NMT",8,1],["NMN",8,1],["UT",10,0],["SM",9,"a"],["SM",9,"b"],["SC",10,0],["STORE",8],["UT",10,1],["SM",9,"c"],["SC",10,1],["SH",10,0],["MXT",11,0],["STT",10,0],["MXT",11,1],["STT",10,1],["A",11,0],["SH",10,1],["STN",10,0],["A",11,1],["MXN",11,0],["SM",9,"d"],["MXN",11,1],["STN",10,1],["SM",9,"q"],["SM",9,"e"],["SC",11,0],["SM",9,"f"],["SM",10,"a"],["SM",10,"b"],["SH",11,0],["SC",11,1],["NMT",9,0],["NMT",9,1],["UT",11,0],["NMN",9,0],["NMN",9,1],["UT",11,1],["SM",10,"c"],["SH",11,1],["STT",11,0],["STORE",9],["STT",11,1],["STN",11,0],["SM",10,"d"],["STN",11,1],["SM",10,"q"],["SM",10,"e"],["SM",11,"a"],["SM",10,"f"],["SM",11,"b"],["NMN",10,0],["NMT",10,0],["NMN",10,1],["SM",11,"c"],["NMT",10,1],["SM",11,"d"],["SM",11,"q"],["STORE",10],["SM",11,"e"],["SM",11,"f"],["NMN",11,0],["NMT",11,0],["NMN",11,1],["NMT",11,1],["STORE",11]]
+ORDER = [["T","w0a",0],["T","w0a",1],["C","w0a",0],["T","w0a",2],["C","w0a",1],["C","w0a",2],["Q","w0a",0],["T","x0",0],["Q","w0a",1],["T","x0",1],["Q","w0a",2],["C","x0",0],["T","x0",2],["C","x0",1],["C","x0",2],["Q","x0",0],["T","x1",0],["Q","x0",1],["T","x1",1],["Q","x0",2],["C","x1",0],["T","x1",2],["C","x1",1],["CONST"],["MXN",0,0],["C","x1",2],["Q","x1",0],["Q","x1",1],["T","w0b",0],["Q","x1",2],["SC",0,0],["T","w0b",1],["C","w0b",0],["T","w0b",2],["C","w0b",1],["T","x2",0],["SH",0,0],["C","w0b",2],["T","x2",1],["MXN",0,1],["C","x2",0],["C","x2",1],["Q","w0b",0],["T","x2",2],["Q","w0b",1],["Q","w0b",2],["T","x3",0],["SC",0,1],["C","x2",2],["MXT",0,0],["Q","x2",0],["C","x3",0],["Q","x2",1],["Q","x2",2],["T","x3",1],["A",0,0],["Q","x3",0],["T","x3",2],["STN",0,0],["SH",0,1],["MXT",0,1],["C","x3",1],["C","x3",2],["T","w1a",0],["Q","x3",1],["A",0,1],["Q","x3",2],["T","w1b",0],["STN",0,1],["MXN",1,0],["C","w1a",0],["C","w1b",0],["Q","w1a",0],["T","w1a",1],["SC",1,0],["T","w1b",1],["C","w1a",1],["Q","w1b",0],["MXN",1,1],["SH",1,0],["C","w1b",1],["T","w1a",2],["SC",1,1],["T","w1b",2],["C","w1a",2],["Q","w1a",1],["UT",0,0],["Q","w1b",1],["UT",0,1],["C","w1b",2],["SH",1,1],["STT",0,0],["MXT",1,0],["STT",0,1],["MXT",1,1],["STN",1,0],["A",1,0],["SM",0,"a"],["T","w2a",0],["SM",0,"b"],["Q","w1a",2],["A",1,1],["SM",0,"c"],["Q","w1b",2],["T","w2b",0],["SM",0,"d"],["MXN",2,0],["STN",1,1],["C","w2a",0],["SM",0,"q"],["C","w2b",0],["Q","w2a",0],["MXN",2,1],["SM",0,"e"],["SC",2,0],["UT",1,0],["SM",0,"f"],["Q","w2b",0],["NMT",0,0],["SH",2,0],["SC",2,1],["T","w2a",1],["T","w2b",1],["STT",1,0],["NMT",0,1],["UT",1,1],["MXT",2,0],["NMN",0,0],["C","w2a",1],["NMN",0,1],["STT",1,1],["SH",2,1],["C","w2b",1],["MXT",2,1],["STORE",0],["A",2,0],["STN",2,0],["T","w2a",2],["A",2,1],["SM",1,"a"],["SM",1,"b"],["T","w2b",2],["Q","w2a",1],["MXN",3,0],["SM",1,"c"],["C","w2a",2],["Q","w2b",1],["SM",1,"d"],["STN",2,1],["C","w2b",2],["MXN",3,1],["Q","w2a",2],["SM",1,"q"],["SC",3,0],["UT",2,0],["SM",1,"e"],["Q","w2b",2],["UT",2,1],["SM",1,"f"],["SH",3,0],["SC",3,1],["MXT",3,0],["NMT",1,0],["STT",2,0],["NMT",1,1],["STT",2,1],["MXT",3,1],["SH",3,1],["STN",3,0],["A",3,0],["T","w3a",0],["SM",2,"a"],["A",3,1],["T","w3b",0],["SM",2,"b"],["NMN",1,0],["MXN",4,0],["C","w3a",0],["SM",2,"c"],["NMN",1,1],["SM",2,"d"],["C","w3b",0],["STN",3,1],["MXN",4,1],["STORE",1],["SM",2,"q"],["SC",4,0],["UT",3,0],["SM",2,"e"],["Q","w3a",0],["T","w3a",1],["SM",2,"f"],["SH",4,0],["SC",4,1],["T","w3b",1],["NMT",2,0],["STT",3,0],["UT",3,1],["MXT",4,0],["NMT",2,1],["STT",3,1],["SH",4,1],["STN",4,0],["C","w3a",1],["MXT",4,1],["A",4,0],["SM",3,"a"],["SM",3,"b"],["T","w3a",2],["Q","w3b",0],["A",4,1],["SM",3,"c"],["Q","w3a",1],["MXN",5,0],["SM",3,"d"],["NMN",2,0],["C","w3b",1],["NMN",2,1],["SM",3,"q"],["MXN",5,1],["STN",4,1],["C","w3a",2],["STORE",2],["SM",3,"e"],["SC",5,0],["T","w3b",2],["SM",3,"f"],["UT",4,0],["SC",5,1],["SH",5,0],["C","w3b",2],["UT",4,1],["STT",4,0],["MXT",5,0],["NMT",3,0],["STT",4,1],["SH",5,1],["NMT",3,1],["MXT",5,1],["STN",5,0],["A",5,0],["SM",4,"a"],["T","w4a",0],["SM",4,"b"],["T","w4b",0],["Q","w3b",1],["A",5,1],["SM",4,"c"],["UT",5,0],["Q","w3a",2],["C","w4a",0],["SM",4,"d"],["Q","w3b",2],["UT",5,1],["NMN",3,0],["SM",4,"q"],["MXN",6,0],["C","w4b",0],["NMN",3,1],["SM",4,"e"],["Q","w4a",0],["STORE",3],["SM",4,"f"],["MXN",6,1],["Q","w4b",0],["NMT",4,0],["SC",6,0],["T","w4a",1],["STN",5,1],["NMT",4,1],["SH",6,0],["T","w4b",1],["SC",6,1],["MXT",6,0],["C","w4a",1],["STT",5,0],["C","w4b",1],["SH",6,1],["MXT",6,1],["STT",5,1],["A",6,0],["STN",6,0],["T","w4a",2],["A",6,1],["SM",5,"a"],["T","w4b",2],["SM",5,"b"],["Q","w4a",1],["MXN",7,0],["C","w4a",2],["SM",5,"c"],["Q","w4b",1],["SM",5,"d"],["NMN",4,0],["C","w4b",2],["Q","w4a",2],["MXN",7,1],["SM",5,"q"],["SC",7,0],["SM",5,"e"],["UT",6,0],["Q","w4b",2],["SM",5,"f"],["SH",7,0],["SC",7,1],["UT",6,1],["NMT",5,0],["MXT",7,0],["STN",6,1],["NMT",5,1],["STT",6,0],["MXT",7,1],["SH",7,1],["STT",6,1],["A",7,0],["T","w5a",0],["STN",7,0],["A",7,1],["T","w5b",0],["SM",6,"a"],["MXN",8,0],["C","w5a",0],["SM",6,"b"],["NMN",4,1],["SM",6,"c"],["NMN",5,0],["C","w5b",0],["STORE",4],["SM",6,"d"],["MXN",8,1],["NMN",5,1],["SM",6,"q"],["SC",8,0],["UT",7,0],["SM",6,"e"],["Q","w5a",0],["T","w5a",1],["SM",6,"f"],["SH",8,0],["SC",8,1],["NMT",6,0],["T","w5b",1],["STN",7,1],["UT",7,1],["STORE",5],["MXT",8,0],["NMT",6,1],["STT",7,0],["SH",8,1],["STT",7,1],["C","w5a",1],["MXT",8,1],["STN",8,0],["A",8,0],["T","w5a",2],["SM",7,"a"],["C","w5b",1],["SM",7,"b"],["Q","w5b",0],["MXN",9,0],["SM",7,"c"],["Q","w5a",1],["A",8,1],["SM",7,"d"],["Q","w5b",1],["SM",7,"q"],["NMN",6,0],["T","w5b",2],["C","w5a",2],["SM",7,"e"],["SC",9,0],["MXN",9,1],["C","w5b",2],["SM",7,"f"],["Q","w5a",2],["NMT",7,0],["NMN",6,1],["UT",8,0],["SH",9,0],["SC",9,1],["UT",8,1],["STORE",6],["NMT",7,1],["MXT",9,0],["STN",8,1],["STT",8,0],["SH",9,1],["MXT",9,1],["A",9,0],["STT",8,1],["STN",9,0],["A",9,1],["MXN",10,0],["SM",8,"a"],["SM",8,"b"],["Q","w5b",2],["MXN",10,1],["SM",8,"c"],["NMN",7,0],["SM",8,"d"],["SC",10,0],["SM",8,"q"],["UT",9,0],["SC",10,1],["UT",9,1],["SH",10,0],["SM",8,"e"],["MXT",10,0],["STN",9,1],["STT",9,0],["MXT",10,1],["SH",10,1],["A",10,0],["STT",9,1],["STN",10,0],["A",10,1],["MXN",11,0],["SM",8,"f"],["SM",9,"a"],["SM",9,"b"],["NMN",7,1],["NMT",8,0],["MXN",11,1],["SM",9,"c"],["SC",11,0],["STORE",7],["NMT",8,1],["SM",9,"d"],["NMN",8,0],["UT",10,0],["SH",11,0],["SC",11,1],["MXT",11,0],["SM",9,"q"],["SM",9,"e"],["STN",10,1],["UT",10,1],["STT",10,0],["A",11,0],["SH",11,1],["MXT",11,1],["STT",10,1],["STN",11,0],["A",11,1],["SM",9,"f"],["SM",10,"a"],["SM",10,"b"],["NMN",8,1],["NMT",9,0],["SM",10,"c"],["NMN",9,0],["STORE",8],["SM",10,"d"],["NMN",9,1],["NMT",9,1],["UT",11,0],["STN",11,1],["SM",10,"q"],["STT",11,0],["UT",11,1],["SM",10,"e"],["STT",11,1],["STORE",9],["SM",10,"f"],["SM",11,"a"],["NMT",10,0],["SM",11,"b"],["NMN",10,0],["SM",11,"c"],["NMN",10,1],["NMT",10,1],["SM",11,"d"],["SM",11,"q"],["SM",11,"e"],["STORE",10],["SM",11,"f"],["NMN",11,0],["NMT",11,0],["NMN",11,1],["NMT",11,1],["STORE",11]]
 
 
 def tile_rebasedlinearattention_pa_kernel(tc, hidden_states, Wq, Wk, gamma, beta, out_0, out_1):
@@ -76,7 +76,13 @@ def tile_rebasedlinearattention_pa_kernel(tc, hidden_states, Wq, Wk, gamma, beta
                 nc.sync.dma_start(out=t[:], in_=w_views[j // 3][:, h0 : h0 + 2, :])
 
         def prep_t(chunk, g):
-            bank = psum_t.tile([P, 2, 2, P], F32, tag="tp", name="tp")
+            early = CHUNKS.index(chunk) < 4
+            if early and g == 1:
+                bank = psum_u.tile([P, 2, 2, P], F32, tag="U", name="tp_u")
+            elif early and g == 2:
+                bank = psum_a.tile([P, 2, 2, P], F32, tag="acc", name="tp_a")
+            else:
+                bank = psum_t.tile([P, 2, 2, P], F32, tag="tp", name="tp")
             tiles[("tp", chunk, g)] = bank
             rows = rows_of(chunk)
             for l in range(2):

@@ -10,316 +10,403 @@ U8 = mybir.dt.uint8
 FP8X4 = mybir.dt.float8_e4m3fn_x4
 ALU = mybir.AluOpType
 ACT = mybir.ActivationFunctionType
-AX = mybir.AxisListType
 
 P = 128
-T = 1024
+TOKENS = 1024
 K = 1536
 D = 128
-NT = T // P
-K_PASS = 512
+TOKEN_TILES = TOKENS // P
+K_PASS = 4 * P
 PASSES = K // K_PASS
+WORDS_PER_PASS = K_PASS // 2
 LN_EPS = 1e-5
-NGROUPS = 6
-NB = 2 * NGROUPS
-N_STATS = 16
+GROUPS_PER_WEIGHT = 3
+BATCHES = 2 * 2 * GROUPS_PER_WEIGHT
+HEAD_TILES = 16
 
-FLOPS = 2 * T * (2 * K) * K
+CHUNKS = [("w", 0), ("x", 0), ("x", 1), ("w", 1), ("x", 2), ("x", 3)] + [("w", n) for n in range(2, 12)]
+FIRST_CHUNKS = 8
 
-PINNED = True
-CHUNKS = ["w0a", "x0", "x1", "w0b", "x2", "x3"] + ["w%d%s" % (j, s) for j in range(1, NGROUPS) for s in "ab"]
-ORDER = [["T","w0a",0],["T","w0a",1],["C","w0a",0],["T","w0a",2],["C","w0a",1],["C","w0a",2],["Q","w0a",0],["T","x0",0],["Q","w0a",1],["T","x0",1],["Q","w0a",2],["C","x0",0],["T","x0",2],["C","x0",1],["C","x0",2],["Q","x0",0],["T","x1",0],["Q","x0",1],["T","x1",1],["Q","x0",2],["C","x1",0],["T","x1",2],["C","x1",1],["CONST"],["MXN",0,0],["C","x1",2],["Q","x1",0],["Q","x1",1],["T","w0b",0],["Q","x1",2],["SC",0,0],["T","w0b",1],["C","w0b",0],["T","w0b",2],["C","w0b",1],["T","x2",0],["SH",0,0],["C","w0b",2],["T","x2",1],["MXN",0,1],["C","x2",0],["C","x2",1],["Q","w0b",0],["T","x2",2],["Q","w0b",1],["Q","w0b",2],["T","x3",0],["SC",0,1],["C","x2",2],["MXT",0,0],["Q","x2",0],["C","x3",0],["Q","x2",1],["Q","x2",2],["T","x3",1],["A",0,0],["Q","x3",0],["T","x3",2],["STN",0,0],["SH",0,1],["MXT",0,1],["C","x3",1],["C","x3",2],["T","w1a",0],["Q","x3",1],["A",0,1],["Q","x3",2],["T","w1b",0],["STN",0,1],["MXN",1,0],["C","w1a",0],["C","w1b",0],["Q","w1a",0],["T","w1a",1],["SC",1,0],["T","w1b",1],["C","w1a",1],["Q","w1b",0],["MXN",1,1],["SH",1,0],["C","w1b",1],["T","w1a",2],["SC",1,1],["T","w1b",2],["C","w1a",2],["Q","w1a",1],["UT",0,0],["Q","w1b",1],["UT",0,1],["C","w1b",2],["SH",1,1],["STT",0,0],["MXT",1,0],["STT",0,1],["MXT",1,1],["STN",1,0],["A",1,0],["SM",0,"a"],["T","w2a",0],["SM",0,"b"],["Q","w1a",2],["A",1,1],["SM",0,"c"],["Q","w1b",2],["T","w2b",0],["SM",0,"d"],["MXN",2,0],["STN",1,1],["C","w2a",0],["SM",0,"q"],["C","w2b",0],["Q","w2a",0],["MXN",2,1],["SM",0,"e"],["SC",2,0],["UT",1,0],["SM",0,"f"],["Q","w2b",0],["NMT",0,0],["SH",2,0],["SC",2,1],["T","w2a",1],["T","w2b",1],["STT",1,0],["NMT",0,1],["UT",1,1],["MXT",2,0],["NMN",0,0],["C","w2a",1],["NMN",0,1],["STT",1,1],["SH",2,1],["C","w2b",1],["MXT",2,1],["STORE",0],["A",2,0],["STN",2,0],["T","w2a",2],["A",2,1],["SM",1,"a"],["SM",1,"b"],["T","w2b",2],["Q","w2a",1],["MXN",3,0],["SM",1,"c"],["C","w2a",2],["Q","w2b",1],["SM",1,"d"],["STN",2,1],["C","w2b",2],["MXN",3,1],["Q","w2a",2],["SM",1,"q"],["SC",3,0],["UT",2,0],["SM",1,"e"],["Q","w2b",2],["UT",2,1],["SM",1,"f"],["SH",3,0],["SC",3,1],["MXT",3,0],["NMT",1,0],["STT",2,0],["NMT",1,1],["STT",2,1],["MXT",3,1],["SH",3,1],["STN",3,0],["A",3,0],["T","w3a",0],["SM",2,"a"],["A",3,1],["T","w3b",0],["SM",2,"b"],["NMN",1,0],["MXN",4,0],["C","w3a",0],["SM",2,"c"],["NMN",1,1],["SM",2,"d"],["C","w3b",0],["STN",3,1],["MXN",4,1],["STORE",1],["SM",2,"q"],["SC",4,0],["UT",3,0],["SM",2,"e"],["Q","w3a",0],["T","w3a",1],["SM",2,"f"],["SH",4,0],["SC",4,1],["T","w3b",1],["NMT",2,0],["STT",3,0],["UT",3,1],["MXT",4,0],["NMT",2,1],["STT",3,1],["SH",4,1],["STN",4,0],["C","w3a",1],["MXT",4,1],["A",4,0],["SM",3,"a"],["SM",3,"b"],["T","w3a",2],["Q","w3b",0],["A",4,1],["SM",3,"c"],["Q","w3a",1],["MXN",5,0],["SM",3,"d"],["NMN",2,0],["C","w3b",1],["NMN",2,1],["SM",3,"q"],["MXN",5,1],["STN",4,1],["C","w3a",2],["STORE",2],["SM",3,"e"],["SC",5,0],["T","w3b",2],["SM",3,"f"],["UT",4,0],["SC",5,1],["SH",5,0],["C","w3b",2],["UT",4,1],["STT",4,0],["MXT",5,0],["NMT",3,0],["STT",4,1],["SH",5,1],["NMT",3,1],["MXT",5,1],["STN",5,0],["A",5,0],["SM",4,"a"],["T","w4a",0],["SM",4,"b"],["T","w4b",0],["Q","w3b",1],["A",5,1],["SM",4,"c"],["UT",5,0],["Q","w3a",2],["C","w4a",0],["SM",4,"d"],["Q","w3b",2],["UT",5,1],["NMN",3,0],["SM",4,"q"],["MXN",6,0],["C","w4b",0],["NMN",3,1],["SM",4,"e"],["Q","w4a",0],["STORE",3],["SM",4,"f"],["MXN",6,1],["Q","w4b",0],["NMT",4,0],["SC",6,0],["T","w4a",1],["STN",5,1],["NMT",4,1],["SH",6,0],["T","w4b",1],["SC",6,1],["MXT",6,0],["C","w4a",1],["STT",5,0],["C","w4b",1],["SH",6,1],["MXT",6,1],["STT",5,1],["A",6,0],["STN",6,0],["T","w4a",2],["A",6,1],["SM",5,"a"],["T","w4b",2],["SM",5,"b"],["Q","w4a",1],["MXN",7,0],["C","w4a",2],["SM",5,"c"],["Q","w4b",1],["SM",5,"d"],["NMN",4,0],["C","w4b",2],["Q","w4a",2],["MXN",7,1],["SM",5,"q"],["SC",7,0],["SM",5,"e"],["UT",6,0],["Q","w4b",2],["SM",5,"f"],["SH",7,0],["SC",7,1],["UT",6,1],["NMT",5,0],["MXT",7,0],["STN",6,1],["NMT",5,1],["STT",6,0],["MXT",7,1],["SH",7,1],["STT",6,1],["A",7,0],["T","w5a",0],["STN",7,0],["A",7,1],["T","w5b",0],["SM",6,"a"],["MXN",8,0],["C","w5a",0],["SM",6,"b"],["NMN",4,1],["SM",6,"c"],["NMN",5,0],["C","w5b",0],["STORE",4],["SM",6,"d"],["MXN",8,1],["NMN",5,1],["SM",6,"q"],["SC",8,0],["UT",7,0],["SM",6,"e"],["Q","w5a",0],["T","w5a",1],["SM",6,"f"],["SH",8,0],["SC",8,1],["NMT",6,0],["T","w5b",1],["STN",7,1],["UT",7,1],["STORE",5],["MXT",8,0],["NMT",6,1],["STT",7,0],["SH",8,1],["STT",7,1],["C","w5a",1],["MXT",8,1],["STN",8,0],["A",8,0],["T","w5a",2],["SM",7,"a"],["C","w5b",1],["SM",7,"b"],["Q","w5b",0],["MXN",9,0],["SM",7,"c"],["Q","w5a",1],["A",8,1],["SM",7,"d"],["Q","w5b",1],["SM",7,"q"],["NMN",6,0],["T","w5b",2],["C","w5a",2],["SM",7,"e"],["SC",9,0],["MXN",9,1],["C","w5b",2],["SM",7,"f"],["Q","w5a",2],["NMT",7,0],["NMN",6,1],["UT",8,0],["SH",9,0],["SC",9,1],["UT",8,1],["STORE",6],["NMT",7,1],["MXT",9,0],["STN",8,1],["STT",8,0],["SH",9,1],["MXT",9,1],["A",9,0],["STT",8,1],["STN",9,0],["A",9,1],["MXN",10,0],["SM",8,"a"],["SM",8,"b"],["Q","w5b",2],["MXN",10,1],["SM",8,"c"],["NMN",7,0],["SM",8,"d"],["SC",10,0],["SM",8,"q"],["UT",9,0],["SC",10,1],["UT",9,1],["SH",10,0],["SM",8,"e"],["MXT",10,0],["STN",9,1],["STT",9,0],["MXT",10,1],["SH",10,1],["A",10,0],["STT",9,1],["STN",10,0],["A",10,1],["MXN",11,0],["SM",8,"f"],["SM",9,"a"],["SM",9,"b"],["NMN",7,1],["NMT",8,0],["MXN",11,1],["SM",9,"c"],["SC",11,0],["STORE",7],["NMT",8,1],["SM",9,"d"],["NMN",8,0],["UT",10,0],["SH",11,0],["SC",11,1],["MXT",11,0],["SM",9,"q"],["SM",9,"e"],["STN",10,1],["UT",10,1],["STT",10,0],["A",11,0],["SH",11,1],["MXT",11,1],["STT",10,1],["STN",11,0],["A",11,1],["SM",9,"f"],["SM",10,"a"],["SM",10,"b"],["NMN",8,1],["NMT",9,0],["SM",10,"c"],["NMN",9,0],["STORE",8],["SM",10,"d"],["NMN",9,1],["NMT",9,1],["UT",11,0],["STN",11,1],["SM",10,"q"],["STT",11,0],["UT",11,1],["SM",10,"e"],["STT",11,1],["STORE",9],["SM",10,"f"],["SM",11,"a"],["NMT",10,0],["SM",11,"b"],["NMN",10,0],["SM",11,"c"],["NMN",10,1],["NMT",10,1],["SM",11,"d"],["SM",11,"q"],["SM",11,"e"],["STORE",10],["SM",11,"f"],["NMN",11,0],["NMT",11,0],["NMN",11,1],["NMT",11,1],["STORE",11]]
+FLOPS = 2 * TOKENS * (2 * K) * K
 
 
 def tile_rebasedlinearattention_pa_kernel(tc, hidden_states, Wq, Wk, gamma, beta, out_0, out_1):
     nc = tc.nc
-    x_view = hidden_states.flatten_outer_dims().rearrange("(p i) k -> p i k", i=NT)
-    w_views = [w.rearrange("(a p) k -> p a k", p=P) for w in (Wq, Wk)]
-    o_views = [
-        o.rearrange("b t h d -> (b t) (h d)").rearrange("(p i) c -> p i c", i=NT) for o in (out_0, out_1)
+    x_view = hidden_states.flatten_outer_dims().rearrange("(p i) k -> p i k", i=TOKEN_TILES)
+    w_views = [w.rearrange("(h p) k -> p h k", p=P) for w in (Wq, Wk)]
+    out_views = [
+        o.rearrange("b t h d -> (b t) (h d)").rearrange("(p i) c -> p i c", i=TOKEN_TILES) for o in (out_0, out_1)
     ]
 
     with ExitStack() as ctx:
-        const = ctx.enter_context(tc.tile_pool(name="const", bufs=1))
-        raw = ctx.enter_context(tc.tile_pool(name="raw", bufs=8))
-        stage = ctx.enter_context(tc.tile_pool(name="stage", bufs=8))
-        wq_pool = ctx.enter_context(tc.tile_pool(name="wq", bufs=3))
-        ut_pool = ctx.enter_context(tc.tile_pool(name="ut", bufs=4))
-        opool = ctx.enter_context(tc.tile_pool(name="o", bufs=5))
-        small = ctx.enter_context(tc.tile_pool(name="small", bufs=3))
-        psum_t = ctx.enter_context(tc.psum_pool(name="psum_t", bufs=2))
-        psum_a = ctx.enter_context(tc.psum_pool(name="psum_a", bufs=2))
-        psum_u = ctx.enter_context(tc.psum_pool(name="psum_u", bufs=4))
-        if PINNED:
-            ctx.enter_context(tc.manual_schedule())
+        keep = ctx.enter_context(tc.tile_pool(name="keep", bufs=1))
+        w_rows = ctx.enter_context(tc.tile_pool(name="w_rows", bufs=8))
+        grouped_pool = ctx.enter_context(tc.tile_pool(name="grouped", bufs=8))
+        w_mx = ctx.enter_context(tc.tile_pool(name="w_mx", bufs=4))
+        turned_pool = ctx.enter_context(tc.tile_pool(name="turned", bufs=4))
+        result_pool = ctx.enter_context(tc.tile_pool(name="result", bufs=5))
+        small = ctx.enter_context(tc.tile_pool(name="small", bufs=4))
+        psum_in = ctx.enter_context(tc.psum_pool(name="psum_in", bufs=2))
+        psum_acc = ctx.enter_context(tc.psum_pool(name="psum_acc", bufs=2))
+        psum_back = ctx.enter_context(tc.psum_pool(name="psum_back", bufs=4))
+        ctx.enter_context(tc.manual_schedule())
 
-        x_raw = const.tile([P, NT, K], BF16)
-        x_codes = const.tile([P, PASSES, T], U32, align_bytes=64)
-        x_scales = const.tile([P, PASSES, T], U8, align_bytes=64)
-        tiles = {}
+        x_rows = keep.tile([P, TOKEN_TILES, K], BF16)
+        x_codes = keep.tile([P, PASSES, TOKENS], U32, align_bytes=64)
+        x_scales = keep.tile([P, PASSES, TOKENS], U8, align_bytes=64)
+        live = {}
 
-        def rows_of(chunk):
-            if chunk[0] == "x":
-                c = int(chunk[1:])
-                return [x_raw[:, 2 * c, :], x_raw[:, 2 * c + 1, :]]
-            return [tiles[("raw", chunk)][:, 0, :], tiles[("raw", chunk)][:, 1, :]]
 
-        def load(chunk):
-            if chunk[0] == "x":
-                c = int(chunk[1:])
-                nc.sync.dma_start(out=x_raw[:, 2 * c : 2 * c + 2, :], in_=x_view[:, 2 * c : 2 * c + 2, :])
+        def load(k):
+            kind, n = CHUNKS[k]
+            if kind == "x":
+                nc.sync.dma_start(out=x_rows[:, 2 * n : 2 * n + 2, :], in_=x_view[:, 2 * n : 2 * n + 2, :])
             else:
-                j = int(chunk[1:-1])
-                h0 = 4 * (j % 3) + (0 if chunk[-1] == "a" else 2)
-                t = raw.tile([P, 2, K], BF16, name="w_raw", tag="w_raw")
-                tiles[("raw", chunk)] = t
-                nc.sync.dma_start(out=t[:], in_=w_views[j // 3][:, h0 : h0 + 2, :])
+                rows = w_rows.tile([P, 2, K], BF16, tag="rows", name="rows")
+                live[("rows", k)] = rows
+                head = 2 * n % 12
+                nc.sync.dma_start(out=rows[:], in_=w_views[n // 6][:, head : head + 2, :])
 
-        def prep_t(chunk, g):
-            early = CHUNKS.index(chunk) < 4
-            if early and g == 1:
-                bank = psum_u.tile([P, 2, 2, P], F32, tag="U", name="tp_u")
-            elif early and g == 2:
-                bank = psum_a.tile([P, 2, 2, P], F32, tag="acc", name="tp_a")
-            else:
-                bank = psum_t.tile([P, 2, 2, P], F32, tag="tp", name="tp")
-            tiles[("tp", chunk, g)] = bank
-            rows = rows_of(chunk)
-            for l in range(2):
-                words = rows[l].bitcast(F32)
+        def transpose_in(k, g, pool):
+            kind, n = CHUNKS[k]
+            source = x_rows[:, 2 * n : 2 * n + 2, :] if kind == "x" else live[("rows", k)][:]
+            bank = pool.tile([P, 2, 2, P], F32, tag="bank", name="in_bank")
+            live[("in", k, g)] = bank
+            for row_tile in range(2):
+                words = source[:, row_tile, :].bitcast(F32)
                 for u in range(2):
-                    c0 = (K_PASS // 2) * g + P * u
-                    nc.tensor.transpose(bank[:, l, u, :], words[:, c0 : c0 + P], ident[:])
+                    first = WORDS_PER_PASS * g + P * u
+                    nc.tensor.transpose(bank[:, row_tile, u, :], words[:, first : first + P], identity[:])
 
-        def prep_c(chunk, g):
-            gr = stage.tile([P, 8 * P], BF16, align_bytes=64, tag="gr", name="gr")
-            tiles[("gr", chunk, g)] = gr
-            dst = gr[:].bitcast(F32).rearrange("p (l r u) -> p l r u", l=2, r=P, u=2)
-            src = tiles[("tp", chunk, g)][:].rearrange("p l u r -> p l r u")
-            if CHUNKS.index(chunk) < 4 and g % 2 == 1:
+        def regroup(k, g, engine):
+            grouped = grouped_pool.tile([P, 2 * P * 4], BF16, align_bytes=64, tag="grouped", name="grouped")
+            live[("grouped", k, g)] = grouped
+            dst = grouped[:].bitcast(F32).rearrange("p (t r u) -> p t r u", t=2, r=P, u=2)
+            src = live[("in", k, g)][:].rearrange("p t u r -> p t r u")
+            if engine == "vector":
                 nc.vector.tensor_copy(out=dst, in_=src)
             else:
                 nc.scalar.copy(out=dst, in_=src)
 
-        def prep_q(chunk, g):
-            if chunk[0] == "x":
-                c = int(chunk[1:])
-                cols = slice(2 * P * c, 2 * P * (c + 1))
+        def quantise(k, g):
+            kind, n = CHUNKS[k]
+            if kind == "x":
                 codes, scales = x_codes, x_scales
+                cols = slice(2 * P * n, 2 * P * (n + 1))
             else:
-                j = int(chunk[1:-1])
-                if ("wc", j) not in tiles:
-                    tiles[("wc", j)] = wq_pool.tile([P, PASSES, 4 * D], U32, align_bytes=64, tag="wc", name="wc")
-                    tiles[("ws", j)] = wq_pool.tile([P, PASSES, 4 * D], U8, align_bytes=64, tag="ws", name="ws")
-                codes, scales = tiles[("wc", j)], tiles[("ws", j)]
-                cols = slice(0, 2 * D) if chunk[-1] == "a" else slice(2 * D, 4 * D)
+                group = n // 2
+                if ("codes", group) not in live:
+                    shape = [P, PASSES, 4 * D]
+                    live[("codes", group)] = w_mx.tile(shape, U32, align_bytes=64, tag="codes", name="w_codes")
+                    live[("scales", group)] = w_mx.tile(shape, U8, align_bytes=64, tag="scales", name="w_scales")
+                codes, scales = live[("codes", group)], live[("scales", group)]
+                cols = slice(2 * D * (n % 2), 2 * D * (n % 2 + 1))
             nc.vector.quantize_mx(
-                out=codes[:, g, cols].bitcast(FP8X4), scales=scales[:, g, cols], in_=tiles[("gr", chunk, g)][:]
+                out=codes[:, g, cols].bitcast(FP8X4), scales=scales[:, g, cols], in_=live[("grouped", k, g)][:]
             )
 
-        def o_tile(b):
-            if ("o", b) not in tiles:
-                tiles[("o", b)] = opool.tile([P, 4, 4 * D], F32, tag="o", name="o")
-            return tiles[("o", b)]
+        def streamed(k):
+            return FIRST_CHUNKS <= k < len(CHUNKS)
 
-        def st_tile(b):
-            if ("st", b) not in tiles:
-                tiles[("st", b)] = small.tile([P, N_STATS, 6], F32, tag="st", name="st")
-            return tiles[("st", b)]
 
-        def mxn(b, u):
-            j, th = b // 2, b % 2
-            acc = psum_a.tile([P, 2, 2 * D], F32, tag="acc", name="acc")
-            tiles[("accn", b, u)] = acc
-            for t2 in range(2):
-                i = 4 * th + 2 * u + t2
-                toks = slice(P * i, P * (i + 1))
-                for g in range(PASSES):
-                    nc.tensor.matmul_mx(
-                        out=acc[:, t2, :],
-                        lhsT=x_codes[:, g, toks].bitcast(FP8X4),
-                        lhsT_scale=x_scales[:, g, toks],
-                        rhs=tiles[("wc", j)][:, g, 0 : 2 * D].bitcast(FP8X4),
-                        rhs_scale=tiles[("ws", j)][:, g, 0 : 2 * D],
-                        start=(g == 0),
-                        stop=(g == PASSES - 1),
-                    )
+        def exists(b):
+            return 0 <= b < BATCHES
 
-        def n_view(b, u):
-            return o_tile(b)[:, 2 * u : 2 * u + 2, 0 : 2 * D].rearrange("p t (h d) -> p t h d", d=D)
+        def result_of(b):
+            if ("result", b) not in live:
+                live[("result", b)] = result_pool.tile([P, 4, 4 * D], F32, tag="result", name="result")
+            return live[("result", b)]
 
-        def sc(b, u):
-            nc.vector.tensor_tensor(
-                out=n_view(b, u),
-                in0=tiles[("accn", b, u)][:].rearrange("p t (h d) -> p t h d", d=D),
-                in1=gb[:, 0:D].unsqueeze(1).unsqueeze(1).to_broadcast([P, 2, 2, D]),
-                op=ALU.mult,
-            )
+        def stats_of(b):
+            if ("stats", b) not in live:
+                live[("stats", b)] = small.tile([P, HEAD_TILES, 6], F32, tag="stats", name="stats")
+            return live[("stats", b)]
 
-        def sh(b, u):
-            nc.gpsimd.tensor_tensor(
-                out=n_view(b, u),
-                in0=n_view(b, u),
-                in1=gb[:, D : 2 * D].unsqueeze(1).unsqueeze(1).to_broadcast([P, 2, 2, D]),
-                op=ALU.add,
-            )
-
-        def stn(b, u):
-            for t2 in range(2):
-                for h in range(2):
-                    nc.vector.bn_stats(
-                        out=st_tile(b)[:, 4 * u + 2 * t2 + h, :], in_=o_tile(b)[:, 2 * u + t2, D * h : D * (h + 1)]
-                    )
-
-        def mxt(b, u):
-            j, th = b // 2, b % 2
-            acc = psum_a.tile([P, 4 * P], F32, tag="acc", name="acc")
-            tiles[("acct", b, u)] = acc
-            feats = slice(D * (2 + u), D * (3 + u))
-            toks = slice(4 * P * th, 4 * P * (th + 1))
+        def product(acc, lhs_codes, lhs_scales, lhs_cols, rhs_codes, rhs_scales, rhs_cols):
             for g in range(PASSES):
                 nc.tensor.matmul_mx(
-                    out=acc[:],
-                    lhsT=tiles[("wc", j)][:, g, feats].bitcast(FP8X4),
-                    lhsT_scale=tiles[("ws", j)][:, g, feats],
-                    rhs=x_codes[:, g, toks].bitcast(FP8X4),
-                    rhs_scale=x_scales[:, g, toks],
+                    out=acc,
+                    lhsT=lhs_codes[:, g, lhs_cols].bitcast(FP8X4),
+                    lhsT_scale=lhs_scales[:, g, lhs_cols],
+                    rhs=rhs_codes[:, g, rhs_cols].bitcast(FP8X4),
+                    rhs_scale=rhs_scales[:, g, rhs_cols],
                     start=(g == 0),
                     stop=(g == PASSES - 1),
                 )
 
-        def affine_t(b, u):
-            ut = ut_pool.tile([P, 4 * P], F32, tag="ut", name="ut")
-            tiles[("ut", b, u)] = ut
-            nc.scalar.activation(
-                out=ut[:], in_=tiles[("acct", b, u)][:], func=ACT.Identity, scale=gcol[:, 0:1], bias=gcol[:, 1:2]
+        def straight_matmuls(b, pair):
+            if not exists(b):
+                return
+            acc = psum_acc.tile([P, 2, 2 * D], F32, tag="bank", name="straight_acc")
+            live[("straight", b, pair)] = acc
+            for t in range(2):
+                i = 4 * (b % 2) + 2 * pair + t
+                product(
+                    acc[:, t, :], x_codes, x_scales, slice(P * i, P * (i + 1)),
+                    live[("codes", b // 2)], live[("scales", b // 2)], slice(0, 2 * D),
+                )
+
+        def straight_view(b, pair):
+            return result_of(b)[:, 2 * pair : 2 * pair + 2, 0 : 2 * D].rearrange("p t (h d) -> p t h d", d=D)
+
+        def times_gamma(b, pair):
+            if not exists(b):
+                return
+            nc.vector.tensor_tensor(
+                out=straight_view(b, pair),
+                in0=live[("straight", b, pair)][:].rearrange("p t (h d) -> p t h d", d=D),
+                in1=affine_rows[:, 0:D].unsqueeze(1).unsqueeze(1).to_broadcast([P, 2, 2, D]),
+                op=ALU.mult,
             )
 
-        def ut_back(b, u):
-            bank = psum_u.tile([P, 4, D], F32, tag="U", name="U")
-            tiles[("U", b, u)] = bank
-            for t in range(4):
-                nc.tensor.transpose(bank[:, t, :], tiles[("ut", b, u)][:, P * t : P * (t + 1)], ident[:])
+        def plus_beta(b, pair):
+            if not exists(b):
+                return
+            nc.gpsimd.tensor_tensor(
+                out=straight_view(b, pair),
+                in0=straight_view(b, pair),
+                in1=affine_rows[:, D : 2 * D].unsqueeze(1).unsqueeze(1).to_broadcast([P, 2, 2, D]),
+                op=ALU.add,
+            )
 
-        def stt(b, u):
-            for t in range(4):
-                nc.vector.bn_stats(out=st_tile(b)[:, 8 + 4 * u + t, :], in_=tiles[("U", b, u)][:, t, :])
-
-        def sm(b, k):
-            n = N_STATS
-            st = st_tile(b)
-            if k == "a":
-                tiles[("sums", b)] = small.tile([P, n, 3], F32, tag="sums", name="sums")
-                nc.vector.tensor_reduce(
-                    out=tiles[("sums", b)][:], in_=st[:].rearrange("p n (a c) -> p n c a", a=2), axis=AX.X, op=ALU.add
-                )
-            elif k == "b":
-                tiles[("diff", b)] = small.tile([P, n], F32, tag="diff", name="diff")
-                nc.vector.tensor_tensor(out=tiles[("diff", b)][:], in0=st[:, :, 1], in1=st[:, :, 4], op=ALU.subtract)
-            elif k == "c":
-                tiles[("dd", b)] = small.tile([P, n], F32, tag="dd", name="dd")
-                nc.vector.scalar_tensor_tensor(
-                    out=tiles[("dd", b)][:],
-                    in0=tiles[("diff", b)][:],
-                    scalar=float(D // 4),
-                    in1=tiles[("diff", b)][:],
-                    op0=ALU.mult,
-                    op1=ALU.mult,
-                )
-            elif k == "d":
-                tiles[("ssq", b)] = small.tile([P, n], F32, tag="ssq", name="ssq")
-                nc.vector.scalar_tensor_tensor(
-                    out=tiles[("ssq", b)][:],
-                    in0=tiles[("sums", b)][:, :, 2],
-                    scalar=D * LN_EPS,
-                    in1=tiles[("dd", b)][:],
-                    op0=ALU.add,
-                    op1=ALU.add,
-                )
-            elif k == "q":
-                tiles[("sd", b)] = small.tile([P, n], F32, tag="sd", name="sd")
-                nc.scalar.activation(
-                    out=tiles[("sd", b)][:],
-                    in_=tiles[("ssq", b)][:],
-                    func=ACT.Sqrt,
-                    scale=(1.0 if b // 2 < 3 else 1.0 / D),
-                )
-            elif k == "e":
-                tiles[("rs", b)] = small.tile([P, n], F32, tag="rs", name="rs")
-                nc.vector.reciprocal(out=tiles[("rs", b)][:], in_=tiles[("sd", b)][:])
-            else:
-                tiles[("nb", b)] = small.tile([P, n], F32, tag="nb", name="nb")
-                nc.vector.scalar_tensor_tensor(
-                    out=tiles[("nb", b)][:],
-                    in0=tiles[("sums", b)][:, :, 1],
-                    scalar=-0.5,
-                    in1=tiles[("rs", b)][:],
-                    op0=ALU.mult,
-                    op1=ALU.mult,
-                )
-
-        def norm(engine, dst, src, b, col):
-            scale = tiles[("rs", b)][:, col : col + 1]
-            bias = tiles[("nb", b)][:, col : col + 1]
-            if engine == "v":
-                nc.vector.tensor_scalar(out=dst, in0=src, scalar1=scale, scalar2=bias, op0=ALU.mult, op1=ALU.add)
-            else:
-                nc.scalar.activation(out=dst, in_=src, func=ACT.Identity, scale=scale, bias=bias)
-
-        def nmn(b, u):
-            for t2 in range(2):
+        def straight_stats(b, pair):
+            if not exists(b):
+                return
+            for t in range(2):
                 for h in range(2):
-                    piece = o_tile(b)[:, 2 * u + t2, D * h : D * (h + 1)]
-                    norm("v", piece, piece, b, 4 * u + 2 * t2 + h)
+                    nc.vector.bn_stats(
+                        out=stats_of(b)[:, 4 * pair + 2 * t + h, :],
+                        in_=result_of(b)[:, 2 * pair + t, D * h : D * (h + 1)],
+                    )
 
-        def nmt(b, u):
+        def turned_matmuls(b, head):
+            if not exists(b):
+                return
+            acc = psum_acc.tile([P, 4 * P], F32, tag="bank", name="turned_acc")
+            live[("turned_acc", b, head)] = acc
+            product(
+                acc[:], live[("codes", b // 2)], live[("scales", b // 2)], slice(D * (2 + head), D * (3 + head)),
+                x_codes, x_scales, slice(4 * P * (b % 2), 4 * P * (b % 2 + 1)),
+            )
+
+        def turned_affine(b, head):
+            if not exists(b):
+                return
+            turned = turned_pool.tile([P, 4 * P], F32, tag="turned", name="turned")
+            live[("turned", b, head)] = turned
+            nc.scalar.activation(
+                out=turned[:],
+                in_=live[("turned_acc", b, head)][:],
+                func=ACT.Identity,
+                scale=affine_cols[:, 0:1],
+                bias=affine_cols[:, 1:2],
+            )
+
+        def turn_back(b, head):
+            if not exists(b):
+                return
+            bank = psum_back.tile([P, 4, D], F32, tag="bank", name="back")
+            live[("back", b, head)] = bank
             for t in range(4):
-                norm("s", o_tile(b)[:, t, D * (2 + u) : D * (3 + u)], tiles[("U", b, u)][:, t, :], b, 8 + 4 * u + t)
+                nc.tensor.transpose(bank[:, t, :], live[("turned", b, head)][:, P * t : P * (t + 1)], identity[:])
+
+        def turned_stats(b, head):
+            if not exists(b):
+                return
+            for t in range(4):
+                nc.vector.bn_stats(out=stats_of(b)[:, 8 + 4 * head + t, :], in_=live[("back", b, head)][:, t, :])
+
+
+        def pair_sums(b):
+            if not exists(b):
+                return
+            live[("sums", b)] = small.tile([P, HEAD_TILES, 3], F32, tag="sums", name="sums")
+            nc.vector.tensor_reduce(
+                out=live[("sums", b)][:],
+                in_=stats_of(b)[:].rearrange("p n (half entry) -> p n entry half", half=2),
+                axis=mybir.AxisListType.X,
+                op=ALU.add,
+            )
+
+        def mean_gap(b):
+            if not exists(b):
+                return
+            live[("gap", b)] = small.tile([P, HEAD_TILES], F32, tag="gap", name="gap")
+            nc.vector.tensor_tensor(
+                out=live[("gap", b)][:], in0=stats_of(b)[:, :, 1], in1=stats_of(b)[:, :, 4], op=ALU.subtract
+            )
+
+        def gap_squared(b):
+            if not exists(b):
+                return
+            live[("gap2", b)] = small.tile([P, HEAD_TILES], F32, tag="gap2", name="gap2")
+            nc.vector.scalar_tensor_tensor(
+                out=live[("gap2", b)][:],
+                in0=live[("gap", b)][:],
+                scalar=D / 4.0,
+                in1=live[("gap", b)][:],
+                op0=ALU.mult,
+                op1=ALU.mult,
+            )
+
+        def spread(b):
+            if not exists(b):
+                return
+            live[("spread", b)] = small.tile([P, HEAD_TILES], F32, tag="spread", name="spread")
+            nc.vector.scalar_tensor_tensor(
+                out=live[("spread", b)][:],
+                in0=live[("sums", b)][:, :, 2],
+                scalar=D * LN_EPS,
+                in1=live[("gap2", b)][:],
+                op0=ALU.add,
+                op1=ALU.add,
+            )
+
+        def factor(b):
+            if not exists(b):
+                return
+            live[("factor", b)] = small.tile([P, HEAD_TILES], F32, tag="factor", name="factor")
+            nc.scalar.activation(
+                out=live[("factor", b)][:],
+                in_=live[("spread", b)][:],
+                func=ACT.Abs_reciprocal_sqrt,
+                scale=(1.0 if b // 2 < GROUPS_PER_WEIGHT else 1.0 / D),
+            )
+
+        def offset(b):
+            if not exists(b):
+                return
+            live[("offset", b)] = small.tile([P, HEAD_TILES], F32, tag="offset", name="offset")
+            nc.vector.scalar_tensor_tensor(
+                out=live[("offset", b)][:],
+                in0=live[("sums", b)][:, :, 1],
+                scalar=-0.5,
+                in1=live[("factor", b)][:],
+                op0=ALU.mult,
+                op1=ALU.mult,
+            )
+
+        def normalise_straight(b, pair):
+            if not exists(b):
+                return
+            for t in range(2):
+                for h in range(2):
+                    n = 4 * pair + 2 * t + h
+                    piece = result_of(b)[:, 2 * pair + t, D * h : D * (h + 1)]
+                    nc.vector.tensor_scalar(
+                        out=piece,
+                        in0=piece,
+                        scalar1=live[("factor", b)][:, n : n + 1],
+                        scalar2=live[("offset", b)][:, n : n + 1],
+                        op0=ALU.mult,
+                        op1=ALU.add,
+                    )
+
+        def normalise_turned(b, head):
+            if not exists(b):
+                return
+            for t in range(4):
+                n = 8 + 4 * head + t
+                nc.scalar.activation(
+                    out=result_of(b)[:, t, D * (2 + head) : D * (3 + head)],
+                    in_=live[("back", b, head)][:, t, :],
+                    func=ACT.Identity,
+                    scale=live[("factor", b)][:, n : n + 1],
+                    bias=live[("offset", b)][:, n : n + 1],
+                )
 
         def store(b):
-            j, th = b // 2, b % 2
-            cols = slice(4 * D * (j % 3), 4 * D * (j % 3 + 1))
-            nc.sync.dma_start(out=o_views[j // 3][:, 4 * th : 4 * th + 4, cols], in_=o_tile(b)[:])
+            if not exists(b):
+                return
+            group, half = b // 2, b % 2
+            cols = slice(4 * D * (group % GROUPS_PER_WEIGHT), 4 * D * (group % GROUPS_PER_WEIGHT + 1))
+            nc.sync.dma_start(
+                out=out_views[group // GROUPS_PER_WEIGHT][:, 4 * half : 4 * half + 4, cols], in_=result_of(b)[:]
+            )
 
-        for chunk in CHUNKS:
-            load(chunk)
-        ident = const.tile([P, P], F32)
-        make_identity(nc, ident[:])
-        ones = const.tile([P, P], BF16)
+
+        for k in range(len(CHUNKS)):
+            load(k)
+        identity = keep.tile([P, P], F32)
+        make_identity(nc, identity[:])
+        ones = keep.tile([P, P], BF16)
         nc.vector.memset(ones[:], 1.0)
-        gb_row = const.tile([P, 2 * D], BF16)
-        nc.vector.memset(gb_row[:], 0.0)
-        warm = const.tile([P, 1], F32)
-        nc.vector.memset(warm[:], 1.0)
-        nc.scalar.dma_start(out=gb_row[0:1, 0:D], in_=gamma.unsqueeze(0))
-        nc.scalar.dma_start(out=gb_row[0:1, D : 2 * D], in_=beta.unsqueeze(0))
-        nc.scalar.activation(out=warm[:], in_=warm[:], func=ACT.Sqrt)
-        gb = const.tile([P, 2 * D], F32)
-        gcol = const.tile([P, 2], F32)
+        gamma_beta = keep.tile([P, 2 * D], BF16)
+        nc.vector.memset(gamma_beta[:], 0.0)
+        one = keep.tile([P, 1], F32)
+        nc.vector.memset(one[:], 1.0)
+        nc.scalar.dma_start(out=gamma_beta[0:1, 0:D], in_=gamma.unsqueeze(0))
+        nc.scalar.dma_start(out=gamma_beta[0:1, D : 2 * D], in_=beta.unsqueeze(0))
+        nc.scalar.activation(out=one[:], in_=one[:], func=ACT.Abs_reciprocal_sqrt)
 
-        def constants():
-            gb_bank = psum_u.tile([P, 2 * D], F32, tag="U", name="gb_bank")
-            nc.tensor.matmul(out=gb_bank[:], lhsT=ones[:], rhs=gb_row[:], start=True, stop=True)
-            nc.scalar.copy(out=gb[:], in_=gb_bank[:])
-            col_bank = psum_u.tile([P, 2, 64], F32, tag="U", name="col_bank")
-            for k in range(2):
-                nc.tensor.matmul(
-                    out=col_bank[:, k, :], lhsT=gb_row[:, D * k : D * (k + 1)], rhs=ones[:, 0:64], start=True, stop=True
-                )
-            nc.scalar.copy(out=gcol[:], in_=col_bank[:, :, 0])
+        early_pools = [psum_in, psum_back, psum_acc, psum_back]
+        for n in range(FIRST_CHUNKS * PASSES):
+            transpose_in(n // PASSES, n % PASSES, early_pools[n % len(early_pools)])
+            regroup(n // PASSES, n % PASSES, "vector" if n % 2 else "scalar")
+            if n > 0:
+                quantise((n - 1) // PASSES, (n - 1) % PASSES)
+        quantise(FIRST_CHUNKS - 1, PASSES - 1)
 
-        kinds = {
-            "T": prep_t, "C": prep_c, "Q": prep_q,
-            "MXN": mxn, "SC": sc, "SH": sh, "STN": stn, "MXT": mxt, "A": affine_t, "UT": ut_back, "STT": stt,
-            "NMN": nmn, "NMT": nmt,
-        }
-        for entry in ORDER:
-            kind = entry[0]
-            if kind == "CONST":
-                constants()
-            elif kind == "SM":
-                sm(entry[1], entry[2])
-            elif kind == "STORE":
-                store(entry[1])
-            else:
-                kinds[kind](entry[1], entry[2])
+        rows_bank = psum_back.tile([P, 2 * D], F32, tag="bank", name="rows_bank")
+        nc.tensor.matmul(out=rows_bank[:], lhsT=ones[:], rhs=gamma_beta[:], start=True, stop=True)
+        affine_rows = keep.tile([P, 2 * D], F32)
+        nc.scalar.copy(out=affine_rows[:], in_=rows_bank[:])
+        cols_bank = psum_back.tile([P, 2, 64], F32, tag="bank", name="cols_bank")
+        for which in range(2):
+            nc.tensor.matmul(
+                out=cols_bank[:, which, :],
+                lhsT=gamma_beta[:, D * which : D * (which + 1)],
+                rhs=ones[:, 0:64],
+                start=True,
+                stop=True,
+            )
+        affine_cols = keep.tile([P, 2], F32)
+        nc.scalar.copy(out=affine_cols[:], in_=cols_bank[:, :, 0])
+
+        for b in range(BATCHES + 3):
+            new, old = b + 7, b + 6
+
+            straight_matmuls(b, 0)
+            turned_matmuls(b - 1, 1)
+            offset(b - 3)
+            if streamed(old):
+                quantise(old, 0)
+            turned_affine(b - 1, 0)
+            if streamed(old):
+                regroup(old, 1, "scalar")
+                regroup(old, 2, "scalar")
+            if streamed(new):
+                transpose_in(new, 0, psum_in)
+            turn_back(b - 1, 0)
+            normalise_turned(b - 3, 0)
+            straight_stats(b - 1, 0)
+            turned_stats(b - 2, 1)
+            times_gamma(b, 0)
+            plus_beta(b, 0)
+            pair_sums(b - 2)
+            mean_gap(b - 2)
+            normalise_straight(b - 3, 0)
+            if streamed(old):
+                quantise(old, 2)
+            gap_squared(b - 2)
+
+            straight_matmuls(b, 1)
+            turned_matmuls(b, 0)
+            if streamed(old):
+                quantise(old, 1)
+            normalise_straight(b - 3, 1)
+            spread(b - 2)
+            turned_affine(b - 1, 1)
+            if streamed(new):
+                transpose_in(new, 1, psum_in)
+            turn_back(b - 1, 1)
+            if streamed(new):
+                transpose_in(new, 2, psum_in)
+                regroup(new, 0, "scalar")
+            normalise_turned(b - 3, 1)
+            store(b - 3)
+            factor(b - 2)
+            straight_stats(b - 1, 1)
+            turned_stats(b - 1, 0)
+            times_gamma(b, 1)
+            plus_beta(b, 1)

@@ -25,7 +25,7 @@ BATCHES = 2 * 2 * GROUPS_PER_WEIGHT
 HEAD_TILES = 16
 
 CHUNKS = [("w", 0), ("x", 0), ("x", 1), ("w", 1), ("x", 2), ("x", 3)] + [("w", n) for n in range(2, 12)]
-FIRST_CHUNKS = 8
+FIRST_CHUNKS = 7
 
 FLOPS = 2 * TOKENS * (2 * K) * K
 

from contextlib import ExitStack

import concourse.mybir as mybir
from concourse.masks import make_identity

F32 = mybir.dt.float32
BF16 = mybir.dt.bfloat16
U32 = mybir.dt.uint32
U8 = mybir.dt.uint8
FP8X4 = mybir.dt.float8_e4m3fn_x4
ALU = mybir.AluOpType
ACT = mybir.ActivationFunctionType

P = 128
TOKENS = 1024
K = 1536
D = 128
TOKEN_TILES = TOKENS // P
K_PASS = 4 * P
PASSES = K // K_PASS
WORDS_PER_PASS = K_PASS // 2
LN_EPS = 1e-5
GROUPS_PER_WEIGHT = 3
BATCHES = 2 * 2 * GROUPS_PER_WEIGHT
HEAD_TILES = 16

CHUNKS = [("w", 0), ("x", 0), ("x", 1), ("w", 1), ("x", 2), ("x", 3)] + [("w", n) for n in range(2, 12)]
FIRST_CHUNKS = 7

FLOPS = 2 * TOKENS * (2 * K) * K


def tile_rebasedlinearattention_pa_kernel(tc, hidden_states, Wq, Wk, gamma, beta, out_0, out_1):
    nc = tc.nc
    x_view = hidden_states.flatten_outer_dims().rearrange("(p i) k -> p i k", i=TOKEN_TILES)
    w_views = [w.rearrange("(h p) k -> p h k", p=P) for w in (Wq, Wk)]
    out_views = [
        o.rearrange("b t h d -> (b t) (h d)").rearrange("(p i) c -> p i c", i=TOKEN_TILES) for o in (out_0, out_1)
    ]

    with ExitStack() as ctx:
        keep = ctx.enter_context(tc.tile_pool(name="keep", bufs=1))
        w_rows = ctx.enter_context(tc.tile_pool(name="w_rows", bufs=8))
        grouped_pool = ctx.enter_context(tc.tile_pool(name="grouped", bufs=8))
        w_mx = ctx.enter_context(tc.tile_pool(name="w_mx", bufs=4))
        turned_pool = ctx.enter_context(tc.tile_pool(name="turned", bufs=4))
        result_pool = ctx.enter_context(tc.tile_pool(name="result", bufs=5))
        small = ctx.enter_context(tc.tile_pool(name="small", bufs=4))
        psum_in = ctx.enter_context(tc.psum_pool(name="psum_in", bufs=2))
        psum_acc = ctx.enter_context(tc.psum_pool(name="psum_acc", bufs=2))
        psum_back = ctx.enter_context(tc.psum_pool(name="psum_back", bufs=4))
        ctx.enter_context(tc.manual_schedule())

        x_rows = keep.tile([P, TOKEN_TILES, K], BF16)
        x_codes = keep.tile([P, PASSES, TOKENS], U32, align_bytes=64)
        x_scales = keep.tile([P, PASSES, TOKENS], U8, align_bytes=64)
        live = {}


        def load(k):
            kind, n = CHUNKS[k]
            if kind == "x":
                nc.sync.dma_start(out=x_rows[:, 2 * n : 2 * n + 2, :], in_=x_view[:, 2 * n : 2 * n + 2, :])
            else:
                rows = w_rows.tile([P, 2, K], BF16, tag="rows", name="rows")
                live[("rows", k)] = rows
                head = 2 * n % 12
                nc.sync.dma_start(out=rows[:], in_=w_views[n // 6][:, head : head + 2, :])

        def transpose_in(k, g, pool):
            kind, n = CHUNKS[k]
            source = x_rows[:, 2 * n : 2 * n + 2, :] if kind == "x" else live[("rows", k)][:]
            bank = pool.tile([P, 2, 2, P], F32, tag="bank", name="in_bank")
            live[("in", k, g)] = bank
            for row_tile in range(2):
                words = source[:, row_tile, :].bitcast(F32)
                for u in range(2):
                    first = WORDS_PER_PASS * g + P * u
                    nc.tensor.transpose(bank[:, row_tile, u, :], words[:, first : first + P], identity[:])

        def regroup(k, g, engine):
            grouped = grouped_pool.tile([P, 2 * P * 4], BF16, align_bytes=64, tag="grouped", name="grouped")
            live[("grouped", k, g)] = grouped
            dst = grouped[:].bitcast(F32).rearrange("p (t r u) -> p t r u", t=2, r=P, u=2)
            src = live[("in", k, g)][:].rearrange("p t u r -> p t r u")
            if engine == "vector":
                nc.vector.tensor_copy(out=dst, in_=src)
            else:
                nc.scalar.copy(out=dst, in_=src)

        def quantise(k, g):
            kind, n = CHUNKS[k]
            if kind == "x":
                codes, scales = x_codes, x_scales
                cols = slice(2 * P * n, 2 * P * (n + 1))
            else:
                group = n // 2
                if ("codes", group) not in live:
                    shape = [P, PASSES, 4 * D]
                    live[("codes", group)] = w_mx.tile(shape, U32, align_bytes=64, tag="codes", name="w_codes")
                    live[("scales", group)] = w_mx.tile(shape, U8, align_bytes=64, tag="scales", name="w_scales")
                codes, scales = live[("codes", group)], live[("scales", group)]
                cols = slice(2 * D * (n % 2), 2 * D * (n % 2 + 1))
            nc.vector.quantize_mx(
                out=codes[:, g, cols].bitcast(FP8X4), scales=scales[:, g, cols], in_=live[("grouped", k, g)][:]
            )

        def streamed(k):
            return FIRST_CHUNKS <= k < len(CHUNKS)


        def exists(b):
            return 0 <= b < BATCHES

        def result_of(b):
            if ("result", b) not in live:
                live[("result", b)] = result_pool.tile([P, 4, 4 * D], F32, tag="result", name="result")
            return live[("result", b)]

        def stats_of(b):
            if ("stats", b) not in live:
                live[("stats", b)] = small.tile([P, HEAD_TILES, 6], F32, tag="stats", name="stats")
            return live[("stats", b)]

        def product(acc, lhs_codes, lhs_scales, lhs_cols, rhs_codes, rhs_scales, rhs_cols):
            for g in range(PASSES):
                nc.tensor.matmul_mx(
                    out=acc,
                    lhsT=lhs_codes[:, g, lhs_cols].bitcast(FP8X4),
                    lhsT_scale=lhs_scales[:, g, lhs_cols],
                    rhs=rhs_codes[:, g, rhs_cols].bitcast(FP8X4),
                    rhs_scale=rhs_scales[:, g, rhs_cols],
                    start=(g == 0),
                    stop=(g == PASSES - 1),
                )

        def straight_matmuls(b, pair):
            if not exists(b):
                return
            acc = psum_acc.tile([P, 2, 2 * D], F32, tag="bank", name="straight_acc")
            live[("straight", b, pair)] = acc
            for t in range(2):
                i = 4 * (b % 2) + 2 * pair + t
                product(
                    acc[:, t, :], x_codes, x_scales, slice(P * i, P * (i + 1)),
                    live[("codes", b // 2)], live[("scales", b // 2)], slice(0, 2 * D),
                )

        def straight_view(b, pair):
            return result_of(b)[:, 2 * pair : 2 * pair + 2, 0 : 2 * D].rearrange("p t (h d) -> p t h d", d=D)

        def times_gamma(b, pair):
            if not exists(b):
                return
            nc.vector.tensor_tensor(
                out=straight_view(b, pair),
                in0=live[("straight", b, pair)][:].rearrange("p t (h d) -> p t h d", d=D),
                in1=affine_rows[:, 0:D].unsqueeze(1).unsqueeze(1).to_broadcast([P, 2, 2, D]),
                op=ALU.mult,
            )

        def plus_beta(b, pair):
            if not exists(b):
                return
            nc.gpsimd.tensor_tensor(
                out=straight_view(b, pair),
                in0=straight_view(b, pair),
                in1=affine_rows[:, D : 2 * D].unsqueeze(1).unsqueeze(1).to_broadcast([P, 2, 2, D]),
                op=ALU.add,
            )

        def straight_stats(b, pair):
            if not exists(b):
                return
            for t in range(2):
                for h in range(2):
                    nc.vector.bn_stats(
                        out=stats_of(b)[:, 4 * pair + 2 * t + h, :],
                        in_=result_of(b)[:, 2 * pair + t, D * h : D * (h + 1)],
                    )

        def turned_matmuls(b, head):
            if not exists(b):
                return
            acc = psum_acc.tile([P, 4 * P], F32, tag="bank", name="turned_acc")
            live[("turned_acc", b, head)] = acc
            product(
                acc[:], live[("codes", b // 2)], live[("scales", b // 2)], slice(D * (2 + head), D * (3 + head)),
                x_codes, x_scales, slice(4 * P * (b % 2), 4 * P * (b % 2 + 1)),
            )

        def turned_affine(b, head):
            if not exists(b):
                return
            turned = turned_pool.tile([P, 4 * P], F32, tag="turned", name="turned")
            live[("turned", b, head)] = turned
            nc.scalar.activation(
                out=turned[:],
                in_=live[("turned_acc", b, head)][:],
                func=ACT.Identity,
                scale=affine_cols[:, 0:1],
                bias=affine_cols[:, 1:2],
            )

        def turn_back(b, head):
            if not exists(b):
                return
            bank = psum_back.tile([P, 4, D], F32, tag="bank", name="back")
            live[("back", b, head)] = bank
            for t in range(4):
                nc.tensor.transpose(bank[:, t, :], live[("turned", b, head)][:, P * t : P * (t + 1)], identity[:])

        def turned_stats(b, head):
            if not exists(b):
                return
            for t in range(4):
                nc.vector.bn_stats(out=stats_of(b)[:, 8 + 4 * head + t, :], in_=live[("back", b, head)][:, t, :])


        def pair_sums(b):
            if not exists(b):
                return
            live[("sums", b)] = small.tile([P, HEAD_TILES, 3], F32, tag="sums", name="sums")
            nc.vector.tensor_reduce(
                out=live[("sums", b)][:],
                in_=stats_of(b)[:].rearrange("p n (half entry) -> p n entry half", half=2),
                axis=mybir.AxisListType.X,
                op=ALU.add,
            )

        def mean_gap(b):
            if not exists(b):
                return
            live[("gap", b)] = small.tile([P, HEAD_TILES], F32, tag="gap", name="gap")
            nc.vector.tensor_tensor(
                out=live[("gap", b)][:], in0=stats_of(b)[:, :, 1], in1=stats_of(b)[:, :, 4], op=ALU.subtract
            )

        def gap_squared(b):
            if not exists(b):
                return
            live[("gap2", b)] = small.tile([P, HEAD_TILES], F32, tag="gap2", name="gap2")
            nc.vector.scalar_tensor_tensor(
                out=live[("gap2", b)][:],
                in0=live[("gap", b)][:],
                scalar=D / 4.0,
                in1=live[("gap", b)][:],
                op0=ALU.mult,
                op1=ALU.mult,
            )

        def spread(b):
            if not exists(b):
                return
            live[("spread", b)] = small.tile([P, HEAD_TILES], F32, tag="spread", name="spread")
            nc.vector.scalar_tensor_tensor(
                out=live[("spread", b)][:],
                in0=live[("sums", b)][:, :, 2],
                scalar=D * LN_EPS,
                in1=live[("gap2", b)][:],
                op0=ALU.add,
                op1=ALU.add,
            )

        def factor(b):
            if not exists(b):
                return
            live[("factor", b)] = small.tile([P, HEAD_TILES], F32, tag="factor", name="factor")
            nc.scalar.activation(
                out=live[("factor", b)][:],
                in_=live[("spread", b)][:],
                func=ACT.Abs_reciprocal_sqrt,
                scale=(1.0 if b // 2 < GROUPS_PER_WEIGHT else 1.0 / D),
            )

        def offset(b):
            if not exists(b):
                return
            live[("offset", b)] = small.tile([P, HEAD_TILES], F32, tag="offset", name="offset")
            nc.vector.scalar_tensor_tensor(
                out=live[("offset", b)][:],
                in0=live[("sums", b)][:, :, 1],
                scalar=-0.5,
                in1=live[("factor", b)][:],
                op0=ALU.mult,
                op1=ALU.mult,
            )

        def normalise_straight(b, pair):
            if not exists(b):
                return
            for t in range(2):
                for h in range(2):
                    n = 4 * pair + 2 * t + h
                    piece = result_of(b)[:, 2 * pair + t, D * h : D * (h + 1)]
                    nc.vector.tensor_scalar(
                        out=piece,
                        in0=piece,
                        scalar1=live[("factor", b)][:, n : n + 1],
                        scalar2=live[("offset", b)][:, n : n + 1],
                        op0=ALU.mult,
                        op1=ALU.add,
                    )

        def normalise_turned(b, head):
            if not exists(b):
                return
            for t in range(4):
                n = 8 + 4 * head + t
                nc.scalar.activation(
                    out=result_of(b)[:, t, D * (2 + head) : D * (3 + head)],
                    in_=live[("back", b, head)][:, t, :],
                    func=ACT.Identity,
                    scale=live[("factor", b)][:, n : n + 1],
                    bias=live[("offset", b)][:, n : n + 1],
                )

        def store(b):
            if not exists(b):
                return
            group, half = b // 2, b % 2
            cols = slice(4 * D * (group % GROUPS_PER_WEIGHT), 4 * D * (group % GROUPS_PER_WEIGHT + 1))
            nc.sync.dma_start(
                out=out_views[group // GROUPS_PER_WEIGHT][:, 4 * half : 4 * half + 4, cols], in_=result_of(b)[:]
            )


        for k in range(len(CHUNKS)):
            load(k)
        identity = keep.tile([P, P], F32)
        make_identity(nc, identity[:])
        ones = keep.tile([P, P], BF16)
        nc.vector.memset(ones[:], 1.0)
        gamma_beta = keep.tile([P, 2 * D], BF16)
        nc.vector.memset(gamma_beta[:], 0.0)
        one = keep.tile([P, 1], F32)
        nc.vector.memset(one[:], 1.0)
        nc.scalar.dma_start(out=gamma_beta[0:1, 0:D], in_=gamma.unsqueeze(0))
        nc.scalar.dma_start(out=gamma_beta[0:1, D : 2 * D], in_=beta.unsqueeze(0))
        nc.scalar.activation(out=one[:], in_=one[:], func=ACT.Abs_reciprocal_sqrt)

        early_pools = [psum_in, psum_back, psum_acc, psum_back]
        for n in range(FIRST_CHUNKS * PASSES):
            transpose_in(n // PASSES, n % PASSES, early_pools[n % len(early_pools)])
            regroup(n // PASSES, n % PASSES, "vector" if n % 2 else "scalar")
            if n > 0:
                quantise((n - 1) // PASSES, (n - 1) % PASSES)
        quantise(FIRST_CHUNKS - 1, PASSES - 1)

        rows_bank = psum_back.tile([P, 2 * D], F32, tag="bank", name="rows_bank")
        nc.tensor.matmul(out=rows_bank[:], lhsT=ones[:], rhs=gamma_beta[:], start=True, stop=True)
        affine_rows = keep.tile([P, 2 * D], F32)
        nc.scalar.copy(out=affine_rows[:], in_=rows_bank[:])
        cols_bank = psum_back.tile([P, 2, 64], F32, tag="bank", name="cols_bank")
        for which in range(2):
            nc.tensor.matmul(
                out=cols_bank[:, which, :],
                lhsT=gamma_beta[:, D * which : D * (which + 1)],
                rhs=ones[:, 0:64],
                start=True,
                stop=True,
            )
        affine_cols = keep.tile([P, 2], F32)
        nc.scalar.copy(out=affine_cols[:], in_=cols_bank[:, :, 0])

        for b in range(BATCHES + 3):
            new, old = b + 7, b + 6

            straight_matmuls(b, 0)
            turned_matmuls(b - 1, 1)
            offset(b - 3)
            if streamed(old):
                quantise(old, 0)
            turned_affine(b - 1, 0)
            if streamed(old):
                regroup(old, 1, "scalar")
                regroup(old, 2, "scalar")
            if streamed(new):
                transpose_in(new, 0, psum_in)
            turn_back(b - 1, 0)
            normalise_turned(b - 3, 0)
            straight_stats(b - 1, 0)
            turned_stats(b - 2, 1)
            times_gamma(b, 0)
            plus_beta(b, 0)
            pair_sums(b - 2)
            mean_gap(b - 2)
            normalise_straight(b - 3, 0)
            if streamed(old):
                quantise(old, 2)
            gap_squared(b - 2)

            straight_matmuls(b, 1)
            turned_matmuls(b, 0)
            if streamed(old):
                quantise(old, 1)
            normalise_straight(b - 3, 1)
            spread(b - 2)
            turned_affine(b - 1, 1)
            if streamed(new):
                transpose_in(new, 1, psum_in)
            turn_back(b - 1, 1)
            if streamed(new):
                transpose_in(new, 2, psum_in)
                regroup(new, 0, "scalar")
            normalise_turned(b - 3, 1)
            store(b - 3)
            factor(b - 2)
            straight_stats(b - 1, 1)
            turned_stats(b - 1, 0)
            times_gamma(b, 1)
            plus_beta(b, 1)
